import numpy as np
import ml_dtypes


def mxq(x, axis, fmt="e4m3"):
    dtype, down = {"e4m3": (ml_dtypes.float8_e4m3fn, 7), "e5m2": (ml_dtypes.float8_e5m2, 14)}[fmt]
    v = np.moveaxis(np.asarray(x, np.float32).astype(ml_dtypes.bfloat16).astype(np.float64), axis, -1)
    blocks = v.reshape(v.shape[:-1] + (-1, 32))
    amax = np.abs(blocks).max(-1, keepdims=True)
    byte = np.maximum(np.where(amax > 0, np.frexp(amax)[1] - 1 + 127, 0) - down, 1)
    scale = np.exp2(byte - 127.0)
    codes = (blocks / scale).astype(np.float32).astype(dtype).astype(np.float64)
    return np.moveaxis((codes * scale).reshape(v.shape), -1, axis)


WIDE = False


def mx_kscale(k):
    if not WIDE:
        return np.ones(k)
    levels = np.array([10, -10, 5, -5, 0])
    a = np.random.permutation(np.resize(levels, k // 512 * 4)).reshape(k // 512, 4)
    idx = np.arange(k)
    return np.exp2(a[idx // 512, idx % 128 // 32])


BF16 = ml_dtypes.bfloat16


def bf(x):
    return np.asarray(x, np.float32).astype(BF16)


def f64(x):
    return np.asarray(x).astype(np.float64)


E2M1 = np.array([0.0, 0.5, 1.0, 1.5, 2.0, 3.0, 4.0, 6.0, -0.0, -0.5, -1.0, -1.5, -2.0, -3.0, -4.0, -6.0])


def pack_weight(w, fmt):
    k, n = w.shape
    w = f64(bf(w)).reshape(k // 32, 32, n)
    amax = np.abs(w).max(1)
    if fmt == "e4m3":
        byte = np.frexp(amax)[1] - 1 + 127 - 7
    else:
        mant, ex = np.frexp(amax / 6.0)
        byte = np.where(mant > 0.5, ex, ex - 1) + 127
    byte = np.clip(np.where(amax > 0, byte, 1), 1, 254)
    scaled = (w * np.exp2(127.0 - byte)[:, None, :]).reshape(k, n).astype(np.float32)
    by_word = np.ascontiguousarray(scaled.reshape(k // 512, 128, 4, n).transpose(0, 1, 3, 2))
    if fmt == "e4m3":
        words = by_word.astype(ml_dtypes.float8_e4m3fn).view(np.uint8)
    else:
        c = by_word.astype(ml_dtypes.float4_e2m1fn).view(np.uint8) & 0xF
        words = c[..., 0::2] | (c[..., 1::2] << 4)
    return np.ascontiguousarray(words), np.ascontiguousarray(byte.astype(np.uint8).reshape(k // 512, 16, n))


def unpack_weight(words, scales, fmt):
    g, p, n, _ = words.shape
    if fmt == "e4m3":
        vals = np.ascontiguousarray(words).view(ml_dtypes.float8_e4m3fn).astype(np.float64)
    else:
        nib = np.empty((g, p, n, 4), np.uint8)
        nib[..., 0::2] = words & 0xF
        nib[..., 1::2] = words >> 4
        vals = E2M1[nib]
    vals = vals * np.repeat(np.exp2(scales.astype(np.float64) - 127.0), 8, axis=1)[..., None]
    return vals.transpose(0, 1, 3, 2).reshape(g * 512, n)


B, C, CQ, CV, H, W = 4, 512, 128, 256, 64, 64
P = H * W
FMT = "e4m3"


def conv1x1(xq, w_words, w_scales, b):
    wt = unpack_weight(w_words, w_scales, FMT)
    y = (wt.T @ xq) + f64(b)[None, :, None]
    return y.reshape(B, wt.shape[1], H, W)


def kronecker(y):
    return np.concatenate([y.mean(axis=3), y.mean(axis=2)], axis=2)


def setup_inputs():
    s = mx_kscale(C)
    g = 3.0 / np.sqrt(C)
    x = bf(np.random.standard_normal((B, C, H, W)) * s[None, :, None, None])
    Wq_words, Wq_scales = pack_weight(np.ascontiguousarray((np.random.standard_normal((CQ, C)) * g / s[None, :]).T), FMT)
    bq = bf(np.random.standard_normal(CQ) * 0.1)
    Wk_words, Wk_scales = pack_weight(np.ascontiguousarray((np.random.standard_normal((CQ, C)) * g / s[None, :]).T), FMT)
    bk = bf(np.random.standard_normal(CQ) * 0.1)
    Wv_words, Wv_scales = pack_weight(np.ascontiguousarray((np.random.standard_normal((CV, C)) * g / s[None, :]).T), FMT)
    bv = bf(np.random.standard_normal(CV) * 0.1)
    return {"x": x,
            "Wq_words": Wq_words, "Wq_scales": Wq_scales,
            "bq": bq,
            "Wk_words": Wk_words, "Wk_scales": Wk_scales,
            "bk": bk,
            "Wv_words": Wv_words, "Wv_scales": Wv_scales,
            "bv": bv}


def reference(x, Wq_words, Wq_scales, bq, Wk_words, Wk_scales, bk, Wv_words, Wv_scales, bv):
    xq = mxq(f64(x).reshape(B, C, P), 1, "e4m3")
    q = kronecker(conv1x1(xq, Wq_words, Wq_scales, bq))
    k = kronecker(conv1x1(xq, Wk_words, Wk_scales, bk))
    v = kronecker(conv1x1(xq, Wv_words, Wv_scales, bv))
    return q, k, v

@@ -1,0 +1,231 @@
+from contextlib import ExitStack
+
+import concourse.mybir as mybir
+from concourse.masks import make_identity
+
+F32 = mybir.dt.float32
+BF16 = mybir.dt.bfloat16
+I32 = mybir.dt.int32
+U32 = mybir.dt.uint32
+U8 = mybir.dt.uint8
+FP8X4 = mybir.dt.float8_e4m3fn_x4
+ADD = mybir.AluOpType.add
+MULT = mybir.AluOpType.mult
+X_AXIS = mybir.AxisListType.X
+
+IMAGES = 4
+CHANNELS = 512
+SIDE = 64
+P = 128
+PACK = 4
+assert CHANNELS == P * PACK
+
+O_TILES = 4
+O_ALL = O_TILES * P
+
+BAND_ROWS = 8
+BAND = BAND_ROWS * SIDE
+BANDS_PER_IMAGE = SIDE // BAND_ROWS
+BANDS = IMAGES * BANDS_PER_IMAGE
+COMBS = 4
+COMB = BAND // COMBS
+CELLS_PER_ROW = SIDE // COMBS
+
+QUANTISE_AHEAD = 2
+REGROUP_AHEAD = 3
+RAW_BUFS = 6
+VECTOR_COMBS = 1
+
+FLOPS = 2 * IMAGES * SIDE * SIDE * CHANNELS * O_ALL
+
+
+def tile_pam_module_pa_t_kernel(
+    tc, x, wq_words, wq_scales, bq, wk_words, wk_scales, bk, wv_words, wv_scales, bv, out_q, out_k, out_v
+):
+    nc = tc.nc
+    with ExitStack() as stack:
+        stack.enter_context(tc.manual_schedule())
+        keep = stack.enter_context(tc.tile_pool(name="keep", bufs=1))
+        raw_pool = stack.enter_context(tc.tile_pool(name="raw", bufs=RAW_BUFS))
+        grouped_pool = stack.enter_context(tc.tile_pool(name="grouped", bufs=3))
+        mx_pool = stack.enter_context(tc.tile_pool(name="mx", bufs=QUANTISE_AHEAD + 3))
+        out_pool = stack.enter_context(tc.tile_pool(name="out", bufs=2))
+        over_rows_psum = stack.enter_context(tc.psum_pool(name="over_rows", bufs=1))
+        over_cols_psum = stack.enter_context(tc.psum_pool(name="over_cols", bufs=3))
+        bias_psum = stack.enter_context(tc.psum_pool(name="bias", bufs=1))
+
+        raw_of = {}
+        grouped_of = {}
+        codes_of = {}
+        scales_of = {}
+        over_cols_of = {}
+        over_rows_of = {}
+        sums_of = {}
+
+        w_codes = keep.tile([P, O_ALL], U32, align_bytes=64)
+        w_scales = keep.tile([P, O_ALL], U8, align_bytes=64)
+        bias_rows = keep.tile([P, P], BF16)
+        bias_cols = keep.tile([P, O_TILES], F32)
+        identity = keep.tile([P, P], BF16)
+
+        def load_biases():
+            nc.vector.memset(bias_rows[:], 0.0)
+            nc.scalar.dma_start(out=bias_rows[0:1, :], in_=bq.rearrange("(r o) -> r o", r=1))
+            nc.scalar.dma_start(out=bias_rows[1:2, :], in_=bk.rearrange("(r o) -> r o", r=1))
+            nc.scalar.dma_start(out=bias_rows[2:4, :], in_=bv.rearrange("(r o) -> r o", r=2))
+            make_identity(nc, identity[:])
+
+        def spread_biases():
+            transposed = bias_psum.tile([P, P], BF16)
+            nc.tensor.transpose(transposed[:], bias_rows[:], identity[:])
+            nc.vector.tensor_copy(out=bias_cols[:], in_=transposed[:, 0:O_TILES])
+
+        def load_weights():
+            nc.vector.memset(w_scales[:].bitcast(I32), 0)
+            first = 0
+            for words, scales in ((wq_words, wq_scales), (wk_words, wk_scales), (wv_words, wv_scales)):
+                cols = slice(first, first + words.shape[2])
+                nc.sync.dma_start(
+                    out=w_codes[:, cols].bitcast(I32),
+                    in_=words[0].rearrange("p n t -> p (n t)").bitcast(I32),
+                )
+                for quadrant in range(4):
+                    nc.sync.dma_start(
+                        out=w_scales[32 * quadrant : 32 * quadrant + 4, cols].bitcast(I32),
+                        in_=scales[0, 4 * quadrant : 4 * quadrant + 4, :].bitcast(I32),
+                    )
+                first += words.shape[2]
+
+        def load(w):
+            if not 0 <= w < BANDS:
+                return
+            image, band = divmod(w, BANDS_PER_IMAGE)
+            raw = raw_pool.tile([P, PACK, BAND], BF16)
+            rows = slice(band * BAND_ROWS, (band + 1) * BAND_ROWS)
+            nc.sync.dma_start(out=raw[:], in_=x[image, :, rows, :].rearrange("(p t) i j -> p t (i j)", t=PACK))
+            raw_of[w] = raw
+
+        def regroup(w):
+            if not 0 <= w < BANDS:
+                return
+            grouped = grouped_pool.tile([P, COMBS, COMB, PACK], BF16, align_bytes=64)
+            by_comb = raw_of[w][:].rearrange("p t (m q) -> p q m t", q=COMBS)
+            nc.vector.tensor_copy(out=grouped[:, 0:VECTOR_COMBS], in_=by_comb[:, 0:VECTOR_COMBS])
+            nc.scalar.copy(out=grouped[:, VECTOR_COMBS:COMBS], in_=by_comb[:, VECTOR_COMBS:COMBS])
+            grouped_of[w] = grouped
+
+        def quantise(w):
+            if not 0 <= w < BANDS:
+                return
+            codes = mx_pool.tile([P, BAND], U32, align_bytes=64)
+            scales = mx_pool.tile([P, BAND], U8, align_bytes=64)
+            nc.vector.quantize_mx(
+                out=codes[:].bitcast(FP8X4),
+                scales=scales[:],
+                in_=grouped_of[w][:].rearrange("p q m t -> p (q m t)"),
+            )
+            codes_of[w] = codes
+            scales_of[w] = scales
+
+        def multiply(w):
+            if not 0 <= w < BANDS:
+                return
+            band = w % BANDS_PER_IMAGE
+            codes = codes_of[w]
+            scales = scales_of[w]
+            if band == 0:
+                for o in range(O_TILES):
+                    over_rows_of[o] = over_rows_psum.tile([P, BAND], F32, name="over_rows_%d" % o)
+            over_cols = over_cols_psum.tile([P, O_TILES, COMB], F32)
+            over_cols_of[w] = over_cols
+
+            def one_pass(out, o, pixels, start, stop):
+                outputs = slice(o * P, (o + 1) * P)
+                nc.tensor.matmul_mx(
+                    out=out,
+                    lhsT=w_codes[:, outputs].bitcast(FP8X4),
+                    lhsT_scale=w_scales[:, outputs],
+                    rhs=codes[:, pixels].bitcast(FP8X4),
+                    rhs_scale=scales[:, pixels],
+                    start=start,
+                    stop=stop,
+                )
+
+            def sum_over_rows():
+                for o in range(O_TILES):
+                    one_pass(over_rows_of[o][:], o, slice(0, BAND), band == 0, band == BANDS_PER_IMAGE - 1)
+
+            def sum_over_cols():
+                for o in range(O_TILES):
+                    for q in range(COMBS):
+                        one_pass(over_cols[:, o, :], o, slice(q * COMB, (q + 1) * COMB), q == 0, q == COMBS - 1)
+
+            if band % 2 == 0:
+                sum_over_cols()
+                sum_over_rows()
+            else:
+                sum_over_rows()
+                sum_over_cols()
+
+        def pool_over_cols(w):
+            if not 0 <= w < BANDS:
+                return
+            image, band = divmod(w, BANDS_PER_IMAGE)
+            if band == 0:
+                sums_of[image] = out_pool.tile([P, O_TILES, 2 * SIDE], F32, name="sums")
+            nc.vector.tensor_reduce(
+                out=sums_of[image][:, :, band * BAND_ROWS : (band + 1) * BAND_ROWS],
+                in_=over_cols_of[w][:].rearrange("p o (i l) -> p o i l", l=CELLS_PER_ROW),
+                axis=X_AXIS,
+                op=ADD,
+            )
+
+        def pool_over_rows(w):
+            if not (0 <= w < BANDS and w % BANDS_PER_IMAGE == BANDS_PER_IMAGE - 1):
+                return
+            for o in range(O_TILES):
+                nc.vector.tensor_reduce(
+                    out=sums_of[w // BANDS_PER_IMAGE][:, o, SIDE : 2 * SIDE].rearrange("p (l q) -> p l q", q=COMBS),
+                    in_=over_rows_of[o][:].rearrange("p (q i l) -> p l q i", q=COMBS, i=BAND_ROWS),
+                    axis=X_AXIS,
+                    op=ADD,
+                )
+
+        def finish(w):
+            if not (0 <= w < BANDS and w % BANDS_PER_IMAGE == BANDS_PER_IMAGE - 1):
+                return
+            image = w // BANDS_PER_IMAGE
+            pooled = out_pool.tile([P, O_TILES, 2 * SIDE], F32)
+            nc.vector.scalar_tensor_tensor(
+                out=pooled[:],
+                in0=sums_of[image][:],
+                scalar=1.0 / SIDE,
+                in1=bias_cols[:].unsqueeze(2).to_broadcast([P, O_TILES, 2 * SIDE]),
+                op0=MULT,
+                op1=ADD,
+            )
+            nc.sync.dma_start(out=out_q[image], in_=pooled[:, 0, :])
+            nc.sync.dma_start(out=out_k[image], in_=pooled[:, 1, :])
+            nc.sync.dma_start(out=out_v[image].rearrange("(h p) c -> p h c", p=P), in_=pooled[:, 2:4, :])
+
+        load_biases()
+        load(0)
+        load(1)
+        load_weights()
+        for w in range(2, RAW_BUFS):
+            load(w)
+
+        def step(w):
+            pool_over_cols(w - 1)
+            finish(w - 1)
+            multiply(w)
+            regroup(w + REGROUP_AHEAD)
+            load(w + REGROUP_AHEAD + RAW_BUFS)
+            quantise(w + QUANTISE_AHEAD)
+            pool_over_rows(w)
+
+        for w in range(-REGROUP_AHEAD, 0):
+            step(w)
+        spread_biases()
+        for w in range(0, BANDS + 1):
+            step(w)

@@ -34,7 +34,7 @@ CELLS_PER_ROW = SIDE // COMBS
 QUANTISE_AHEAD = 2
 REGROUP_AHEAD = 3
 RAW_BUFS = 6
-VECTOR_COMBS = 1
+VECTOR_PLACES = 32
 
 FLOPS = 2 * IMAGES * SIDE * SIDE * CHANNELS * O_ALL
 
@@ -109,9 +109,10 @@ def tile_pam_module_pa_t_kernel(
             if not 0 <= w < BANDS:
                 return
             grouped = grouped_pool.tile([P, COMBS, COMB, PACK], BF16, align_bytes=64)
-            by_comb = raw_of[w][:].rearrange("p t (m q) -> p q m t", q=COMBS)
-            nc.vector.tensor_copy(out=grouped[:, 0:VECTOR_COMBS], in_=by_comb[:, 0:VECTOR_COMBS])
-            nc.scalar.copy(out=grouped[:, VECTOR_COMBS:COMBS], in_=by_comb[:, VECTOR_COMBS:COMBS])
+            source = raw_of[w][:].rearrange("p t (m q) -> p m t q", q=COMBS)
+            target = grouped[:].rearrange("p q m t -> p m t q")
+            nc.vector.tensor_copy(out=target[:, 0:VECTOR_PLACES], in_=source[:, 0:VECTOR_PLACES])
+            nc.scalar.copy(out=target[:, VECTOR_PLACES:COMB], in_=source[:, VECTOR_PLACES:COMB])
             grouped_of[w] = grouped
 
         def quantise(w):

@@ -34,7 +34,7 @@ CELLS_PER_ROW = SIDE // COMBS
 QUANTISE_AHEAD = 2
 REGROUP_AHEAD = 3
 RAW_BUFS = 6
-VECTOR_PLACES = 32
+VECTOR_PLACES = 64
 
 FLOPS = 2 * IMAGES * SIDE * SIDE * CHANNELS * O_ALL
 

@@ -31,10 +31,10 @@ COMBS = 4
 COMB = BAND // COMBS
 CELLS_PER_ROW = SIDE // COMBS
 
-QUANTISE_AHEAD = 2
-REGROUP_AHEAD = 3
+QUANTISE_AHEAD = 3
+REGROUP_AHEAD = 4
 RAW_BUFS = 6
-VECTOR_PLACES = 64
+VECTOR_PLACES = 48
 
 FLOPS = 2 * IMAGES * SIDE * SIDE * CHANNELS * O_ALL
 
@@ -50,9 +50,8 @@ def tile_pam_module_pa_t_kernel(
         grouped_pool = stack.enter_context(tc.tile_pool(name="grouped", bufs=3))
         mx_pool = stack.enter_context(tc.tile_pool(name="mx", bufs=QUANTISE_AHEAD + 3))
         out_pool = stack.enter_context(tc.tile_pool(name="out", bufs=2))
-        over_rows_psum = stack.enter_context(tc.psum_pool(name="over_rows", bufs=1))
-        over_cols_psum = stack.enter_context(tc.psum_pool(name="over_cols", bufs=3))
-        bias_psum = stack.enter_context(tc.psum_pool(name="bias", bufs=1))
+        over_rows_psum = stack.enter_context(tc.psum_pool(name="over_rows_psum", bufs=5))
+        over_cols_psum = stack.enter_context(tc.psum_pool(name="over_cols_psum", bufs=3))
 
         raw_of = {}
         grouped_of = {}
@@ -70,31 +69,27 @@ def tile_pam_module_pa_t_kernel(
 
         def load_biases():
             nc.vector.memset(bias_rows[:], 0.0)
-            nc.scalar.dma_start(out=bias_rows[0:1, :], in_=bq.rearrange("(r o) -> r o", r=1))
-            nc.scalar.dma_start(out=bias_rows[1:2, :], in_=bk.rearrange("(r o) -> r o", r=1))
-            nc.scalar.dma_start(out=bias_rows[2:4, :], in_=bv.rearrange("(r o) -> r o", r=2))
+            nc.sync.dma_start(out=bias_rows[0:1, :], in_=bq.rearrange("(r o) -> r o", r=1))
+            nc.sync.dma_start(out=bias_rows[1:2, :], in_=bk.rearrange("(r o) -> r o", r=1))
+            nc.sync.dma_start(out=bias_rows[2:4, :], in_=bv.rearrange("(r o) -> r o", r=2))
             make_identity(nc, identity[:])
 
         def spread_biases():
-            transposed = bias_psum.tile([P, P], BF16)
+            transposed = over_cols_psum.tile([P, P], BF16, tag="over_cols")
             nc.tensor.transpose(transposed[:], bias_rows[:], identity[:])
             nc.vector.tensor_copy(out=bias_cols[:], in_=transposed[:, 0:O_TILES])
 
-        def load_weights():
-            nc.vector.memset(w_scales[:].bitcast(I32), 0)
-            first = 0
-            for words, scales in ((wq_words, wq_scales), (wk_words, wk_scales), (wv_words, wv_scales)):
-                cols = slice(first, first + words.shape[2])
+        def load_weight(words, scales, first):
+            cols = slice(first, first + words.shape[2])
+            nc.sync.dma_start(
+                out=w_codes[:, cols].bitcast(I32),
+                in_=words[0].rearrange("p n t -> p (n t)").bitcast(I32),
+            )
+            for quadrant in range(4):
                 nc.sync.dma_start(
-                    out=w_codes[:, cols].bitcast(I32),
-                    in_=words[0].rearrange("p n t -> p (n t)").bitcast(I32),
+                    out=w_scales[32 * quadrant : 32 * quadrant + 4, cols].bitcast(I32),
+                    in_=scales[0, 4 * quadrant : 4 * quadrant + 4, :].bitcast(I32),
                 )
-                for quadrant in range(4):
-                    nc.sync.dma_start(
-                        out=w_scales[32 * quadrant : 32 * quadrant + 4, cols].bitcast(I32),
-                        in_=scales[0, 4 * quadrant : 4 * quadrant + 4, :].bitcast(I32),
-                    )
-                first += words.shape[2]
 
         def load(w):
             if not 0 <= w < BANDS:
@@ -136,7 +131,7 @@ def tile_pam_module_pa_t_kernel(
             scales = scales_of[w]
             if band == 0:
                 for o in range(O_TILES):
-                    over_rows_of[o] = over_rows_psum.tile([P, BAND], F32, name="over_rows_%d" % o)
+                    over_rows_of[o] = over_rows_psum.tile([P, BAND], F32, name="over_rows")
             over_cols = over_cols_psum.tile([P, O_TILES, COMB], F32)
             over_cols_of[w] = over_cols
 
@@ -152,21 +147,10 @@ def tile_pam_module_pa_t_kernel(
                     stop=stop,
                 )
 
-            def sum_over_rows():
-                for o in range(O_TILES):
-                    one_pass(over_rows_of[o][:], o, slice(0, BAND), band == 0, band == BANDS_PER_IMAGE - 1)
-
-            def sum_over_cols():
-                for o in range(O_TILES):
-                    for q in range(COMBS):
-                        one_pass(over_cols[:, o, :], o, slice(q * COMB, (q + 1) * COMB), q == 0, q == COMBS - 1)
-
-            if band % 2 == 0:
-                sum_over_cols()
-                sum_over_rows()
-            else:
-                sum_over_rows()
-                sum_over_cols()
+            for o in range(O_TILES):
+                one_pass(over_rows_of[o][:], o, slice(0, BAND), band == 0, band == BANDS_PER_IMAGE - 1)
+                for q in range(COMBS):
+                    one_pass(over_cols[:, o, :], o, slice(q * COMB, (q + 1) * COMB), q == 0, q == COMBS - 1)
 
         def pool_over_cols(w):
             if not 0 <= w < BANDS:
@@ -209,24 +193,27 @@ def tile_pam_module_pa_t_kernel(
             nc.sync.dma_start(out=out_k[image], in_=pooled[:, 1, :])
             nc.sync.dma_start(out=out_v[image].rearrange("(h p) c -> p h c", p=P), in_=pooled[:, 2:4, :])
 
-        load_biases()
+        nc.vector.memset(w_scales[:].bitcast(I32), 0)
         load(0)
         load(1)
-        load_weights()
+        load_weight(wq_words, wq_scales, 0)
+        load_weight(wk_words, wk_scales, P)
+        load_weight(wv_words, wv_scales, 2 * P)
         for w in range(2, RAW_BUFS):
             load(w)
+        load_biases()
 
         def step(w):
             pool_over_cols(w - 1)
             finish(w - 1)
             multiply(w)
+            quantise(w + QUANTISE_AHEAD)
             regroup(w + REGROUP_AHEAD)
             load(w + REGROUP_AHEAD + RAW_BUFS)
-            quantise(w + QUANTISE_AHEAD)
             pool_over_rows(w)
 
-        for w in range(-REGROUP_AHEAD, 0):
+        for w in range(-REGROUP_AHEAD, BANDS_PER_IMAGE):
             step(w)
         spread_biases()
-        for w in range(0, BANDS + 1):
+        for w in range(BANDS_PER_IMAGE, BANDS + 1):
             step(w)

@@ -12,6 +12,7 @@ FP8X4 = mybir.dt.float8_e4m3fn_x4
 ADD = mybir.AluOpType.add
 MULT = mybir.AluOpType.mult
 X_AXIS = mybir.AxisListType.X
+IDENTITY = mybir.ActivationFunctionType.Identity
 
 IMAGES = 4
 CHANNELS = 512
@@ -34,6 +35,9 @@ CELLS_PER_ROW = SIDE // COMBS
 QUANTISE_AHEAD = 3
 REGROUP_AHEAD = 4
 RAW_BUFS = 6
+LAST_BANDS = 2
+HEAD_PIECES = 2
+HEAD_VECTOR_PLACES = 42
 VECTOR_PLACES = 48
 
 FLOPS = 2 * IMAGES * SIDE * SIDE * CHANNELS * O_ALL
@@ -96,8 +100,14 @@ def tile_pam_module_pa_t_kernel(
                 return
             image, band = divmod(w, BANDS_PER_IMAGE)
             raw = raw_pool.tile([P, PACK, BAND], BF16)
-            rows = slice(band * BAND_ROWS, (band + 1) * BAND_ROWS)
-            nc.sync.dma_start(out=raw[:], in_=x[image, :, rows, :].rearrange("(p t) i j -> p t (i j)", t=PACK))
+            pieces = HEAD_PIECES if w == 0 else 1
+            rows = BAND_ROWS // pieces
+            for n in range(pieces):
+                first = band * BAND_ROWS + n * rows
+                nc.sync.dma_start(
+                    out=raw[:, :, n * rows * SIDE : (n + 1) * rows * SIDE],
+                    in_=x[image, :, first : first + rows, :].rearrange("(p t) i j -> p t (i j)", t=PACK),
+                )
             raw_of[w] = raw
 
         def regroup(w):
@@ -106,8 +116,12 @@ def tile_pam_module_pa_t_kernel(
             grouped = grouped_pool.tile([P, COMBS, COMB, PACK], BF16, align_bytes=64)
             source = raw_of[w][:].rearrange("p t (m q) -> p m t q", q=COMBS)
             target = grouped[:].rearrange("p q m t -> p m t q")
-            nc.vector.tensor_copy(out=target[:, 0:VECTOR_PLACES], in_=source[:, 0:VECTOR_PLACES])
-            nc.scalar.copy(out=target[:, VECTOR_PLACES:COMB], in_=source[:, VECTOR_PLACES:COMB])
+            pieces, vector_places = (HEAD_PIECES, HEAD_VECTOR_PLACES) if w == 0 else (1, VECTOR_PLACES)
+            for n in range(pieces):
+                first, end = n * COMB // pieces, (n + 1) * COMB // pieces
+                cut = first + vector_places
+                nc.vector.tensor_copy(out=target[:, first:cut], in_=source[:, first:cut])
+                nc.scalar.copy(out=target[:, cut:end], in_=source[:, cut:end])
             grouped_of[w] = grouped
 
         def quantise(w):
@@ -123,37 +137,48 @@ def tile_pam_module_pa_t_kernel(
             codes_of[w] = codes
             scales_of[w] = scales
 
-        def multiply(w):
-            if not 0 <= w < BANDS:
-                return
+        def one_pass(out, w, o, pixels, start, stop):
+            outputs = slice(o * P, (o + 1) * P)
+            nc.tensor.matmul_mx(
+                out=out,
+                lhsT=w_codes[:, outputs].bitcast(FP8X4),
+                lhsT_scale=w_scales[:, outputs],
+                rhs=codes_of[w][:, pixels].bitcast(FP8X4),
+                rhs_scale=scales_of[w][:, pixels],
+                start=start,
+                stop=stop,
+            )
+
+        def add_rows(w, o):
             band = w % BANDS_PER_IMAGE
-            codes = codes_of[w]
-            scales = scales_of[w]
-            if band == 0:
+            one_pass(over_rows_of[o][:], w, o, slice(0, BAND), band == 0, band == BANDS_PER_IMAGE - 1)
+
+        def add_cols(out, w, o):
+            for q in range(COMBS):
+                one_pass(out, w, o, slice(q * COMB, (q + 1) * COMB), q == 0, q == COMBS - 1)
+
+        def multiply(w):
+            if not 0 <= w < BANDS - LAST_BANDS:
+                return
+            if w % BANDS_PER_IMAGE == 0:
                 for o in range(O_TILES):
                     over_rows_of[o] = over_rows_psum.tile([P, BAND], F32, name="over_rows")
-            over_cols = over_cols_psum.tile([P, O_TILES, COMB], F32)
+            over_cols = over_cols_psum.tile([P, O_TILES, COMB], F32, tag="over_cols")
             over_cols_of[w] = over_cols
-
-            def one_pass(out, o, pixels, start, stop):
-                outputs = slice(o * P, (o + 1) * P)
-                nc.tensor.matmul_mx(
-                    out=out,
-                    lhsT=w_codes[:, outputs].bitcast(FP8X4),
-                    lhsT_scale=w_scales[:, outputs],
-                    rhs=codes[:, pixels].bitcast(FP8X4),
-                    rhs_scale=scales[:, pixels],
-                    start=start,
-                    stop=stop,
-                )
-
             for o in range(O_TILES):
-                one_pass(over_rows_of[o][:], o, slice(0, BAND), band == 0, band == BANDS_PER_IMAGE - 1)
-                for q in range(COMBS):
-                    one_pass(over_cols[:, o, :], o, slice(q * COMB, (q + 1) * COMB), q == 0, q == COMBS - 1)
+                add_rows(w, o)
+                add_cols(over_cols[:, o, :], w, o)
+
+        def multiply_last(o):
+            over_cols = over_cols_psum.tile([P, LAST_BANDS, COMB], F32, tag="over_cols")
+            over_cols_of["last", o] = over_cols
+            for w in range(BANDS - LAST_BANDS, BANDS):
+                add_rows(w, o)
+            for n in range(LAST_BANDS):
+                add_cols(over_cols[:, n, :], BANDS - LAST_BANDS + n, o)
 
         def pool_over_cols(w):
-            if not 0 <= w < BANDS:
+            if not 0 <= w < BANDS - LAST_BANDS:
                 return
             image, band = divmod(w, BANDS_PER_IMAGE)
             if band == 0:
@@ -165,19 +190,22 @@ def tile_pam_module_pa_t_kernel(
                 op=ADD,
             )
 
+        def pool_tile_over_rows(image, o):
+            nc.vector.tensor_reduce(
+                out=sums_of[image][:, o, SIDE : 2 * SIDE].rearrange("p (l q) -> p l q", q=COMBS),
+                in_=over_rows_of[o][:].rearrange("p (q i l) -> p l q i", q=COMBS, i=BAND_ROWS),
+                axis=X_AXIS,
+                op=ADD,
+            )
+
         def pool_over_rows(w):
-            if not (0 <= w < BANDS and w % BANDS_PER_IMAGE == BANDS_PER_IMAGE - 1):
+            if not (0 <= w < BANDS - LAST_BANDS and w % BANDS_PER_IMAGE == BANDS_PER_IMAGE - 1):
                 return
             for o in range(O_TILES):
-                nc.vector.tensor_reduce(
-                    out=sums_of[w // BANDS_PER_IMAGE][:, o, SIDE : 2 * SIDE].rearrange("p (l q) -> p l q", q=COMBS),
-                    in_=over_rows_of[o][:].rearrange("p (q i l) -> p l q i", q=COMBS, i=BAND_ROWS),
-                    axis=X_AXIS,
-                    op=ADD,
-                )
+                pool_tile_over_rows(w // BANDS_PER_IMAGE, o)
 
         def finish(w):
-            if not (0 <= w < BANDS and w % BANDS_PER_IMAGE == BANDS_PER_IMAGE - 1):
+            if not (0 <= w < BANDS - LAST_BANDS and w % BANDS_PER_IMAGE == BANDS_PER_IMAGE - 1):
                 return
             image = w // BANDS_PER_IMAGE
             pooled = out_pool.tile([P, O_TILES, 2 * SIDE], F32)
@@ -193,10 +221,29 @@ def tile_pam_module_pa_t_kernel(
             nc.sync.dma_start(out=out_k[image], in_=pooled[:, 1, :])
             nc.sync.dma_start(out=out_v[image].rearrange("(h p) c -> p h c", p=P), in_=pooled[:, 2:4, :])
 
+        def pool_last(o):
+            image = IMAGES - 1
+            pool_tile_over_rows(image, o)
+            nc.vector.tensor_reduce(
+                out=sums_of[image][:, o, SIDE - LAST_BANDS * BAND_ROWS : SIDE],
+                in_=over_cols_of["last", o][:].rearrange("p b (i l) -> p (b i) l", l=CELLS_PER_ROW),
+                axis=X_AXIS,
+                op=ADD,
+            )
+
+        def finish_last(o):
+            image = IMAGES - 1
+            pooled = out_pool.tile([P, 2 * SIDE], F32, name="pooled_tile")
+            nc.scalar.activation(
+                out=pooled[:], in_=sums_of[image][:, o, :], func=IDENTITY, bias=bias_cols[:, o : o + 1], scale=1.0 / SIDE
+            )
+            target = (out_q[image], out_k[image], out_v[image, 0:P, :], out_v[image, P : 2 * P, :])[o]
+            nc.sync.dma_start(out=target, in_=pooled[:])
+
         nc.vector.memset(w_scales[:].bitcast(I32), 0)
         load(0)
-        load(1)
         load_weight(wq_words, wq_scales, 0)
+        load(1)
         load_weight(wk_words, wk_scales, P)
         load_weight(wv_words, wv_scales, 2 * P)
         for w in range(2, RAW_BUFS):
@@ -215,5 +262,9 @@ def tile_pam_module_pa_t_kernel(
         for w in range(-REGROUP_AHEAD, BANDS_PER_IMAGE):
             step(w)
         spread_biases()
-        for w in range(BANDS_PER_IMAGE, BANDS + 1):
+        for w in range(BANDS_PER_IMAGE, BANDS - LAST_BANDS + 1):
             step(w)
+        for o in range(O_TILES):
+            multiply_last(o)
+            pool_last(o)
+            finish_last(o)

@@ -23,6 +23,7 @@ assert CHANNELS == P * PACK
 
 O_TILES = 4
 O_ALL = O_TILES * P
+SCALE_PITCH = 256
 
 BAND_ROWS = 8
 BAND = BAND_ROWS * SIDE
@@ -65,8 +66,8 @@ def tile_pam_module_pa_t_kernel(
         over_rows_of = {}
         sums_of = {}
 
-        w_codes = keep.tile([P, O_ALL], U32, align_bytes=64)
-        w_scales = keep.tile([P, O_ALL], U8, align_bytes=64)
+        w_codes = keep.tile([P, O_ALL], U32, align_bytes=256)
+        w_scales = keep.tile([P, O_TILES, SCALE_PITCH], U8, align_bytes=256)
         bias_rows = keep.tile([P, P], BF16)
         bias_cols = keep.tile([P, O_TILES], F32)
         identity = keep.tile([P, P], BF16)
@@ -85,14 +86,15 @@ def tile_pam_module_pa_t_kernel(
 
         def load_weight(words, scales, first):
             cols = slice(first, first + words.shape[2])
+            tiles = slice(first // P, (first + words.shape[2]) // P)
             nc.sync.dma_start(
                 out=w_codes[:, cols].bitcast(I32),
                 in_=words[0].rearrange("p n t -> p (n t)").bitcast(I32),
             )
             for quadrant in range(4):
                 nc.sync.dma_start(
-                    out=w_scales[32 * quadrant : 32 * quadrant + 4, cols].bitcast(I32),
-                    in_=scales[0, 4 * quadrant : 4 * quadrant + 4, :].bitcast(I32),
+                    out=w_scales[32 * quadrant : 32 * quadrant + 4, tiles, 0:P].bitcast(I32),
+                    in_=scales[0, 4 * quadrant : 4 * quadrant + 4, :].bitcast(I32).rearrange("r (o n) -> r o n", n=P // 4),
                 )
 
         def load(w):
@@ -127,8 +129,8 @@ def tile_pam_module_pa_t_kernel(
         def quantise(w):
             if not 0 <= w < BANDS:
                 return
-            codes = mx_pool.tile([P, BAND], U32, align_bytes=64)
-            scales = mx_pool.tile([P, BAND], U8, align_bytes=64)
+            codes = mx_pool.tile([P, BAND], U32, align_bytes=256)
+            scales = mx_pool.tile([P, BAND], U8, align_bytes=256)
             nc.vector.quantize_mx(
                 out=codes[:].bitcast(FP8X4),
                 scales=scales[:],
@@ -142,7 +144,7 @@ def tile_pam_module_pa_t_kernel(
             nc.tensor.matmul_mx(
                 out=out,
                 lhsT=w_codes[:, outputs].bitcast(FP8X4),
-                lhsT_scale=w_scales[:, outputs],
+                lhsT_scale=w_scales[:, o, 0:P],
                 rhs=codes_of[w][:, pixels].bitcast(FP8X4),
                 rhs_scale=scales_of[w][:, pixels],
                 start=start,
@@ -240,7 +242,7 @@ def tile_pam_module_pa_t_kernel(
             target = (out_q[image], out_k[image], out_v[image, 0:P, :], out_v[image, P : 2 * P, :])[o]
             nc.sync.dma_start(out=target, in_=pooled[:])
 
-        nc.vector.memset(w_scales[:].bitcast(I32), 0)
+        nc.vector.memset(w_scales[:].rearrange("p o n -> p (o n)").bitcast(I32), 0)
         load(0)
         load_weight(wq_words, wq_scales, 0)
         load(1)

@@ -33,12 +33,15 @@ COMBS = 4
 COMB = BAND // COMBS
 CELLS_PER_ROW = SIDE // COMBS
 
+FIRST_DOUBLE = 8
+PAIR = 2
 QUANTISE_AHEAD = 3
 REGROUP_AHEAD = 4
 RAW_BUFS = 6
 LAST_BANDS = 2
 HEAD_PIECES = 2
 HEAD_VECTOR_PLACES = 42
+WARM_UP_PASSES = 8
 VECTOR_PLACES = 48
 
 FLOPS = 2 * IMAGES * SIDE * SIDE * CHANNELS * O_ALL
@@ -97,6 +100,18 @@ def tile_pam_module_pa_t_kernel(
                     in_=scales[0, 4 * quadrant : 4 * quadrant + 4, :].bitcast(I32).rearrange("r (o n) -> r o n", n=P // 4),
                 )
 
+        def warm_up():
+            zeros = keep.tile([P, BAND], BF16)
+            nc.vector.memset(zeros[:], 0.0)
+            unused = over_cols_psum.tile([P, BAND], F32, tag="over_cols")
+            for n in range(WARM_UP_PASSES):
+                nc.tensor.matmul(unused[:], lhsT=zeros[:, 0:P], rhs=zeros[:], start=True, stop=True)
+
+        def group_of(w):
+            if FIRST_DOUBLE <= w < BANDS - LAST_BANDS:
+                return w - (w - FIRST_DOUBLE) % PAIR, PAIR
+            return w, 1
+
         def load(w):
             if not 0 <= w < BANDS:
                 return
@@ -106,7 +121,8 @@ def tile_pam_module_pa_t_kernel(
             rows = BAND_ROWS // pieces
             for n in range(pieces):
                 first = band * BAND_ROWS + n * rows
-                nc.sync.dma_start(
+                queue = (nc.scalar, nc.gpsimd)[w] if w < 2 else nc.sync
+                queue.dma_start(
                     out=raw[:, :, n * rows * SIDE : (n + 1) * rows * SIDE],
                     in_=x[image, :, first : first + rows, :].rearrange("(p t) i j -> p t (i j)", t=PACK),
                 )
@@ -115,29 +131,34 @@ def tile_pam_module_pa_t_kernel(
         def regroup(w):
             if not 0 <= w < BANDS:
                 return
-            grouped = grouped_pool.tile([P, COMBS, COMB, PACK], BF16, align_bytes=64)
+            first_band, bands = group_of(w)
+            if w == first_band:
+                grouped_of[w] = grouped_pool.tile([P, COMBS, bands * COMB, PACK], BF16, align_bytes=64, name="grouped")
+            here = slice((w - first_band) * COMB, (w - first_band + 1) * COMB)
             source = raw_of[w][:].rearrange("p t (m q) -> p m t q", q=COMBS)
-            target = grouped[:].rearrange("p q m t -> p m t q")
+            target = grouped_of[first_band][:, :, here, :].rearrange("p q m t -> p m t q")
             pieces, vector_places = (HEAD_PIECES, HEAD_VECTOR_PLACES) if w == 0 else (1, VECTOR_PLACES)
             for n in range(pieces):
                 first, end = n * COMB // pieces, (n + 1) * COMB // pieces
                 cut = first + vector_places
                 nc.vector.tensor_copy(out=target[:, first:cut], in_=source[:, first:cut])
                 nc.scalar.copy(out=target[:, cut:end], in_=source[:, cut:end])
-            grouped_of[w] = grouped
 
         def quantise(w):
             if not 0 <= w < BANDS:
                 return
-            codes = mx_pool.tile([P, BAND], U32, align_bytes=256)
-            scales = mx_pool.tile([P, BAND], U8, align_bytes=256)
+            first_band, bands = group_of(w)
+            if w != first_band + bands - 1:
+                return
+            codes = mx_pool.tile([P, bands * BAND], U32, align_bytes=256)
+            scales = mx_pool.tile([P, bands * BAND], U8, align_bytes=256)
             nc.vector.quantize_mx(
                 out=codes[:].bitcast(FP8X4),
                 scales=scales[:],
-                in_=grouped_of[w][:].rearrange("p q m t -> p (q m t)"),
+                in_=grouped_of[first_band][:].rearrange("p q m t -> p (q m t)"),
             )
-            codes_of[w] = codes
-            scales_of[w] = scales
+            codes_of[first_band] = codes
+            scales_of[first_band] = scales
 
         def one_pass(out, w, o, pixels, start, stop):
             outputs = slice(o * P, (o + 1) * P)
@@ -151,25 +172,45 @@ def tile_pam_module_pa_t_kernel(
                 stop=stop,
             )
 
+        def row_passes(bands):
+            if bands == 1:
+                return [(0, 0, BAND)]
+            passes = [(COMB, 0, 2 * COMB), (5 * COMB, 2 * COMB, 2 * COMB)]
+            return passes + [(0, 0, COMB), (3 * COMB, COMB, 2 * COMB), (7 * COMB, 3 * COMB, COMB)]
+
         def add_rows(w, o):
-            band = w % BANDS_PER_IMAGE
-            one_pass(over_rows_of[o][:], w, o, slice(0, BAND), band == 0, band == BANDS_PER_IMAGE - 1)
+            bands = group_of(w)[1]
+            image_start = w % BANDS_PER_IMAGE == 0
+            image_end = (w + bands) % BANDS_PER_IMAGE == 0
+            if image_start:
+                over_rows_of[o] = over_rows_psum.tile([P, BAND], F32, name="over_rows")
+            passes = row_passes(bands)
+            for n, (first, cell, width) in enumerate(passes):
+                one_pass(
+                    over_rows_of[o][:, cell : cell + width],
+                    w,
+                    o,
+                    slice(first, first + width),
+                    image_start and n == 0,
+                    image_end and n == len(passes) - 1,
+                )
 
         def add_cols(out, w, o):
+            comb = group_of(w)[1] * COMB
             for q in range(COMBS):
-                one_pass(out, w, o, slice(q * COMB, (q + 1) * COMB), q == 0, q == COMBS - 1)
+                one_pass(out, w, o, slice(q * comb, (q + 1) * comb), q == 0, q == COMBS - 1)
 
         def multiply(w):
             if not 0 <= w < BANDS - LAST_BANDS:
                 return
-            if w % BANDS_PER_IMAGE == 0:
-                for o in range(O_TILES):
-                    over_rows_of[o] = over_rows_psum.tile([P, BAND], F32, name="over_rows")
-            over_cols = over_cols_psum.tile([P, O_TILES, COMB], F32, tag="over_cols")
+            first_band, bands = group_of(w)
+            tiles = O_TILES // bands
+            over_cols = over_cols_psum.tile([P, tiles, bands * COMB], F32, tag="over_cols")
             over_cols_of[w] = over_cols
-            for o in range(O_TILES):
-                add_rows(w, o)
-                add_cols(over_cols[:, o, :], w, o)
+            for n in range(tiles):
+                o = (w - first_band) * tiles + n
+                add_rows(first_band, o)
+                add_cols(over_cols[:, n, :], first_band, o)
 
         def multiply_last(o):
             over_cols = over_cols_psum.tile([P, LAST_BANDS, COMB], F32, tag="over_cols")
@@ -183,10 +224,14 @@ def tile_pam_module_pa_t_kernel(
             if not 0 <= w < BANDS - LAST_BANDS:
                 return
             image, band = divmod(w, BANDS_PER_IMAGE)
+            first_band, bands = group_of(w)
             if band == 0:
                 sums_of[image] = out_pool.tile([P, O_TILES, 2 * SIDE], F32, name="sums")
+            tiles = O_TILES // bands
+            first_tile = (w - first_band) * tiles
+            first_row = (first_band % BANDS_PER_IMAGE) * BAND_ROWS
             nc.vector.tensor_reduce(
-                out=sums_of[image][:, :, band * BAND_ROWS : (band + 1) * BAND_ROWS],
+                out=sums_of[image][:, first_tile : first_tile + tiles, first_row : first_row + bands * BAND_ROWS],
                 in_=over_cols_of[w][:].rearrange("p o (i l) -> p o i l", l=CELLS_PER_ROW),
                 axis=X_AXIS,
                 op=ADD,
@@ -201,10 +246,13 @@ def tile_pam_module_pa_t_kernel(
             )
 
         def pool_over_rows(w):
-            if not (0 <= w < BANDS - LAST_BANDS and w % BANDS_PER_IMAGE == BANDS_PER_IMAGE - 1):
+            if not 0 <= w < BANDS - LAST_BANDS:
                 return
-            for o in range(O_TILES):
-                pool_tile_over_rows(w // BANDS_PER_IMAGE, o)
+            first_band, bands = group_of(w)
+            if (first_band + bands) % BANDS_PER_IMAGE == 0:
+                tiles = O_TILES // bands
+                for n in range(tiles):
+                    pool_tile_over_rows(w // BANDS_PER_IMAGE, (w - first_band) * tiles + n)
 
         def finish(w):
             if not (0 <= w < BANDS - LAST_BANDS and w % BANDS_PER_IMAGE == BANDS_PER_IMAGE - 1):
@@ -242,6 +290,7 @@ def tile_pam_module_pa_t_kernel(
             target = (out_q[image], out_k[image], out_v[image, 0:P, :], out_v[image, P : 2 * P, :])[o]
             nc.sync.dma_start(out=target, in_=pooled[:])
 
+        warm_up()
         nc.vector.memset(w_scales[:].rearrange("p o n -> p (o n)").bitcast(I32), 0)
         load(0)
         load_weight(wq_words, wq_scales, 0)

@@ -42,7 +42,7 @@ LAST_BANDS = 2
 HEAD_PIECES = 2
 HEAD_VECTOR_PLACES = 42
 WARM_UP_PASSES = 8
-VECTOR_PLACES = 48
+VECTOR_PLACES = 32
 
 FLOPS = 2 * IMAGES * SIDE * SIDE * CHANNELS * O_ALL
 

@@ -41,8 +41,12 @@ RAW_BUFS = 6
 LAST_BANDS = 2
 HEAD_PIECES = 2
 HEAD_VECTOR_PLACES = 42
+HEAD_BANDS = 4
+HALF_PLACES = COMB // 2
 WARM_UP_PASSES = 8
-VECTOR_PLACES = 32
+VECTOR_PLACES = 24
+DERIVED = 2
+DERIVED_IMAGES = (1, 2)
 
 FLOPS = 2 * IMAGES * SIDE * SIDE * CHANNELS * O_ALL
 
@@ -67,6 +71,7 @@ def tile_pam_module_pa_t_kernel(
         scales_of = {}
         over_cols_of = {}
         over_rows_of = {}
+        parts_of = {}
         sums_of = {}
 
         w_codes = keep.tile([P, O_ALL], U32, align_bytes=256)
@@ -121,7 +126,7 @@ def tile_pam_module_pa_t_kernel(
             rows = BAND_ROWS // pieces
             for n in range(pieces):
                 first = band * BAND_ROWS + n * rows
-                queue = (nc.scalar, nc.gpsimd)[w] if w < 2 else nc.sync
+                queue = nc.scalar if w == 0 else nc.gpsimd if w < HEAD_BANDS else nc.sync
                 queue.dma_start(
                     out=raw[:, :, n * rows * SIDE : (n + 1) * rows * SIDE],
                     in_=x[image, :, first : first + rows, :].rearrange("(p t) i j -> p t (i j)", t=PACK),
@@ -137,7 +142,8 @@ def tile_pam_module_pa_t_kernel(
             here = slice((w - first_band) * COMB, (w - first_band + 1) * COMB)
             source = raw_of[w][:].rearrange("p t (m q) -> p m t q", q=COMBS)
             target = grouped_of[first_band][:, :, here, :].rearrange("p q m t -> p m t q")
-            pieces, vector_places = (HEAD_PIECES, HEAD_VECTOR_PLACES) if w == 0 else (1, VECTOR_PLACES)
+            pieces = HEAD_PIECES if w == 0 else 1
+            vector_places = HEAD_VECTOR_PLACES if w == 0 else HALF_PLACES if w < HEAD_BANDS else VECTOR_PLACES
             for n in range(pieces):
                 first, end = n * COMB // pieces, (n + 1) * COMB // pieces
                 cut = first + vector_places
@@ -172,11 +178,16 @@ def tile_pam_module_pa_t_kernel(
                 stop=stop,
             )
 
-        def row_passes(bands):
+        def is_derived(image, o):
+            return image in DERIVED_IMAGES and o < DERIVED
+
+        def row_passes(bands, combs):
             if bands == 1:
                 return [(0, 0, BAND)]
-            passes = [(COMB, 0, 2 * COMB), (5 * COMB, 2 * COMB, 2 * COMB)]
-            return passes + [(0, 0, COMB), (3 * COMB, COMB, 2 * COMB), (7 * COMB, 3 * COMB, COMB)]
+            if combs == COMBS:
+                passes = [(COMB, 0, 2 * COMB), (5 * COMB, 2 * COMB, 2 * COMB)]
+                return passes + [(0, 0, COMB), (3 * COMB, COMB, 2 * COMB), (7 * COMB, 3 * COMB, COMB)]
+            return [(COMB, 0, 2 * COMB), (5 * COMB, 2 * COMB, COMB), (0, 0, COMB), (3 * COMB, COMB, 2 * COMB)]
 
         def add_rows(w, o):
             bands = group_of(w)[1]
@@ -184,7 +195,7 @@ def tile_pam_module_pa_t_kernel(
             image_end = (w + bands) % BANDS_PER_IMAGE == 0
             if image_start:
                 over_rows_of[o] = over_rows_psum.tile([P, BAND], F32, name="over_rows")
-            passes = row_passes(bands)
+            passes = row_passes(bands, COMBS - 1 if is_derived(w // BANDS_PER_IMAGE, o) else COMBS)
             for n, (first, cell, width) in enumerate(passes):
                 one_pass(
                     over_rows_of[o][:, cell : cell + width],
@@ -236,11 +247,24 @@ def tile_pam_module_pa_t_kernel(
                 axis=X_AXIS,
                 op=ADD,
             )
+            if image in DERIVED_IMAGES and first_tile < DERIVED:
+                if band == 0:
+                    parts_of[image] = out_pool.tile(
+                        [P, BANDS_PER_IMAGE // PAIR, DERIVED, CELLS_PER_ROW], F32, name="parts"
+                    )
+                derived = min(DERIVED - first_tile, tiles)
+                nc.vector.tensor_reduce(
+                    out=parts_of[image][:, band // PAIR, first_tile : first_tile + derived, :],
+                    in_=over_cols_of[w][:, 0:derived, :].rearrange("p o (i l) -> p o l i", l=CELLS_PER_ROW),
+                    axis=X_AXIS,
+                    op=ADD,
+                )
 
         def pool_tile_over_rows(image, o):
+            combs = COMBS - 1 if is_derived(image, o) else COMBS
             nc.vector.tensor_reduce(
-                out=sums_of[image][:, o, SIDE : 2 * SIDE].rearrange("p (l q) -> p l q", q=COMBS),
-                in_=over_rows_of[o][:].rearrange("p (q i l) -> p l q i", q=COMBS, i=BAND_ROWS),
+                out=sums_of[image][:, o, SIDE : 2 * SIDE].rearrange("p (l q) -> p l q", q=COMBS)[:, :, 0:combs],
+                in_=over_rows_of[o][:, 0 : combs * COMB].rearrange("p (q i l) -> p l q i", q=combs, i=BAND_ROWS),
                 axis=X_AXIS,
                 op=ADD,
             )
@@ -253,6 +277,21 @@ def tile_pam_module_pa_t_kernel(
                 tiles = O_TILES // bands
                 for n in range(tiles):
                     pool_tile_over_rows(w // BANDS_PER_IMAGE, (w - first_band) * tiles + n)
+
+        def derive(w):
+            if not (0 <= w < BANDS - LAST_BANDS and w % BANDS_PER_IMAGE == BANDS_PER_IMAGE - 1):
+                return
+            image = w // BANDS_PER_IMAGE
+            if image not in DERIVED_IMAGES:
+                return
+            columns = sums_of[image][:, 0:DERIVED, SIDE : 2 * SIDE].rearrange("p o (l q) -> p o l q", q=COMBS)
+            known = out_pool.tile([P, DERIVED, CELLS_PER_ROW], F32)
+            nc.vector.tensor_reduce(out=known[:], in_=columns[:, :, :, 0 : COMBS - 1], axis=X_AXIS, op=ADD)
+            together = out_pool.tile([P, DERIVED, CELLS_PER_ROW], F32)
+            nc.vector.tensor_reduce(
+                out=together[:], in_=parts_of[image][:].rearrange("p b o l -> p o l b"), axis=X_AXIS, op=ADD
+            )
+            nc.vector.tensor_sub(out=columns[:, :, :, COMBS - 1], in0=together[:], in1=known[:])
 
         def finish(w):
             if not (0 <= w < BANDS - LAST_BANDS and w % BANDS_PER_IMAGE == BANDS_PER_IMAGE - 1):
@@ -294,15 +333,17 @@ def tile_pam_module_pa_t_kernel(
         nc.vector.memset(w_scales[:].rearrange("p o n -> p (o n)").bitcast(I32), 0)
         load(0)
         load_weight(wq_words, wq_scales, 0)
-        load(1)
+        for w in range(1, HEAD_BANDS):
+            load(w)
         load_weight(wk_words, wk_scales, P)
         load_weight(wv_words, wv_scales, 2 * P)
-        for w in range(2, RAW_BUFS):
+        for w in range(HEAD_BANDS, RAW_BUFS):
             load(w)
         load_biases()
 
         def step(w):
             pool_over_cols(w - 1)
+            derive(w - 1)
             finish(w - 1)
             multiply(w)
             quantise(w + QUANTISE_AHEAD)

@@ -44,8 +44,8 @@ HEAD_VECTOR_PLACES = 42
 HEAD_BANDS = 4
 HALF_PLACES = COMB // 2
 WARM_UP_PASSES = 8
-VECTOR_PLACES = 24
-DERIVED = 2
+GPSIMD_PLACES = 16
+DERIVED = 4
 DERIVED_IMAGES = (1, 2)
 
 FLOPS = 2 * IMAGES * SIDE * SIDE * CHANNELS * O_ALL
@@ -117,6 +117,9 @@ def tile_pam_module_pa_t_kernel(
                 return w - (w - FIRST_DOUBLE) % PAIR, PAIR
             return w, 1
 
+        def is_second(w):
+            return group_of(w)[0] < w
+
         def load(w):
             if not 0 <= w < BANDS:
                 return
@@ -143,11 +146,21 @@ def tile_pam_module_pa_t_kernel(
             source = raw_of[w][:].rearrange("p t (m q) -> p m t q", q=COMBS)
             target = grouped_of[first_band][:, :, here, :].rearrange("p q m t -> p m t q")
             pieces = HEAD_PIECES if w == 0 else 1
-            vector_places = HEAD_VECTOR_PLACES if w == 0 else HALF_PLACES if w < HEAD_BANDS else VECTOR_PLACES
+            places = HEAD_VECTOR_PLACES if w == 0 else HALF_PLACES if w < HEAD_BANDS else GPSIMD_PLACES
             for n in range(pieces):
                 first, end = n * COMB // pieces, (n + 1) * COMB // pieces
-                cut = first + vector_places
-                nc.vector.tensor_copy(out=target[:, first:cut], in_=source[:, first:cut])
+                cut = first + places
+                if w < HEAD_BANDS:
+                    nc.vector.tensor_copy(out=target[:, first:cut], in_=source[:, first:cut])
+                else:
+                    nc.gpsimd.tensor_scalar(
+                        out=target[:, first:cut],
+                        in0=source[:, first:cut],
+                        scalar1=1.0,
+                        scalar2=0.0,
+                        op0=MULT,
+                        op1=ADD,
+                    )
                 nc.scalar.copy(out=target[:, cut:end], in_=source[:, cut:end])
 
         def quantise(w):
@@ -343,13 +356,16 @@ def tile_pam_module_pa_t_kernel(
 
         def step(w):
             pool_over_cols(w - 1)
-            derive(w - 1)
-            finish(w - 1)
             multiply(w)
             quantise(w + QUANTISE_AHEAD)
             regroup(w + REGROUP_AHEAD)
             load(w + REGROUP_AHEAD + RAW_BUFS)
-            pool_over_rows(w)
+            if is_second(w - 1):
+                pool_over_rows(w - 1)
+            if not is_second(w):
+                pool_over_rows(w)
+            derive(w - 2)
+            finish(w - 2)
 
         for w in range(-REGROUP_AHEAD, BANDS_PER_IMAGE):
             step(w)

@@ -33,7 +33,7 @@ COMBS = 4
 COMB = BAND // COMBS
 CELLS_PER_ROW = SIDE // COMBS
 
-FIRST_DOUBLE = 8
+FIRST_DOUBLE = 4
 PAIR = 2
 QUANTISE_AHEAD = 3
 REGROUP_AHEAD = 4
@@ -44,9 +44,9 @@ HEAD_VECTOR_PLACES = 42
 HEAD_BANDS = 4
 HALF_PLACES = COMB // 2
 WARM_UP_PASSES = 8
-GPSIMD_PLACES = 16
-DERIVED = 4
-DERIVED_IMAGES = (1, 2)
+GPSIMD_PLACES = 32
+GPSIMD_PIECES = 2
+DERIVED_TILES = (2, 4, 4, 0)
 
 FLOPS = 2 * IMAGES * SIDE * SIDE * CHANNELS * O_ALL
 
@@ -153,14 +153,16 @@ def tile_pam_module_pa_t_kernel(
                 if w < HEAD_BANDS:
                     nc.vector.tensor_copy(out=target[:, first:cut], in_=source[:, first:cut])
                 else:
-                    nc.gpsimd.tensor_scalar(
-                        out=target[:, first:cut],
-                        in0=source[:, first:cut],
-                        scalar1=1.0,
-                        scalar2=0.0,
-                        op0=MULT,
-                        op1=ADD,
-                    )
+                    size = GPSIMD_PLACES // GPSIMD_PIECES
+                    for here in (slice(k * size, (k + 1) * size) for k in range(GPSIMD_PIECES)):
+                        nc.gpsimd.tensor_scalar(
+                            out=target[:, here].rearrange("p m t q -> p m q t"),
+                            in0=source[:, here].rearrange("p m t q -> p m q t"),
+                            scalar1=1.0,
+                            scalar2=0.0,
+                            op0=MULT,
+                            op1=ADD,
+                        )
                 nc.scalar.copy(out=target[:, cut:end], in_=source[:, cut:end])
 
         def quantise(w):
@@ -171,11 +173,16 @@ def tile_pam_module_pa_t_kernel(
                 return
             codes = mx_pool.tile([P, bands * BAND], U32, align_bytes=256)
             scales = mx_pool.tile([P, bands * BAND], U8, align_bytes=256)
-            nc.vector.quantize_mx(
-                out=codes[:].bitcast(FP8X4),
-                scales=scales[:],
-                in_=grouped_of[first_band][:].rearrange("p q m t -> p (q m t)"),
-            )
+            values = grouped_of[first_band][:].rearrange("p q m t -> p (q m t)")
+            pieces = HEAD_PIECES if w == 0 else 1
+            width = bands * BAND // pieces
+            for n in range(pieces):
+                here = slice(n * width, (n + 1) * width)
+                nc.vector.quantize_mx(
+                    out=codes[:, here].bitcast(FP8X4),
+                    scales=scales[:, here],
+                    in_=values[:, n * width * PACK : (n + 1) * width * PACK],
+                )
             codes_of[first_band] = codes
             scales_of[first_band] = scales
 
@@ -191,12 +198,18 @@ def tile_pam_module_pa_t_kernel(
                 stop=stop,
             )
 
-        def is_derived(image, o):
-            return image in DERIVED_IMAGES and o < DERIVED
+        def groups_of(image):
+            bands = range(image * BANDS_PER_IMAGE, (image + 1) * BANDS_PER_IMAGE)
+            return [w for w in bands if group_of(w)[0] == w]
+
+        def combs_over_rows(image, o):
+            return COMBS - 1 if o < DERIVED_TILES[image] else COMBS
 
         def row_passes(bands, combs):
-            if bands == 1:
+            if bands == 1 and combs == COMBS:
                 return [(0, 0, BAND)]
+            if bands == 1:
+                return [(0, 0, 2 * COMB), (2 * COMB, 2 * COMB, COMB)]
             if combs == COMBS:
                 passes = [(COMB, 0, 2 * COMB), (5 * COMB, 2 * COMB, 2 * COMB)]
                 return passes + [(0, 0, COMB), (3 * COMB, COMB, 2 * COMB), (7 * COMB, 3 * COMB, COMB)]
@@ -208,7 +221,7 @@ def tile_pam_module_pa_t_kernel(
             image_end = (w + bands) % BANDS_PER_IMAGE == 0
             if image_start:
                 over_rows_of[o] = over_rows_psum.tile([P, BAND], F32, name="over_rows")
-            passes = row_passes(bands, COMBS - 1 if is_derived(w // BANDS_PER_IMAGE, o) else COMBS)
+            passes = row_passes(bands, combs_over_rows(w // BANDS_PER_IMAGE, o))
             for n, (first, cell, width) in enumerate(passes):
                 one_pass(
                     over_rows_of[o][:, cell : cell + width],
@@ -233,8 +246,12 @@ def tile_pam_module_pa_t_kernel(
             over_cols_of[w] = over_cols
             for n in range(tiles):
                 o = (w - first_band) * tiles + n
-                add_rows(first_band, o)
-                add_cols(over_cols[:, n, :], first_band, o)
+                if w == 0:
+                    add_cols(over_cols[:, n, :], first_band, o)
+                    add_rows(first_band, o)
+                else:
+                    add_rows(first_band, o)
+                    add_cols(over_cols[:, n, :], first_band, o)
 
         def multiply_last(o):
             over_cols = over_cols_psum.tile([P, LAST_BANDS, COMB], F32, tag="over_cols")
@@ -260,21 +277,22 @@ def tile_pam_module_pa_t_kernel(
                 axis=X_AXIS,
                 op=ADD,
             )
-            if image in DERIVED_IMAGES and first_tile < DERIVED:
+            derived = min(DERIVED_TILES[image] - first_tile, tiles)
+            if derived > 0:
+                groups = groups_of(image)
                 if band == 0:
                     parts_of[image] = out_pool.tile(
-                        [P, BANDS_PER_IMAGE // PAIR, DERIVED, CELLS_PER_ROW], F32, name="parts"
+                        [P, len(groups), DERIVED_TILES[image], CELLS_PER_ROW], F32, name="parts"
                     )
-                derived = min(DERIVED - first_tile, tiles)
                 nc.vector.tensor_reduce(
-                    out=parts_of[image][:, band // PAIR, first_tile : first_tile + derived, :],
+                    out=parts_of[image][:, groups.index(first_band), first_tile : first_tile + derived, :],
                     in_=over_cols_of[w][:, 0:derived, :].rearrange("p o (i l) -> p o l i", l=CELLS_PER_ROW),
                     axis=X_AXIS,
                     op=ADD,
                 )
 
         def pool_tile_over_rows(image, o):
-            combs = COMBS - 1 if is_derived(image, o) else COMBS
+            combs = combs_over_rows(image, o)
             nc.vector.tensor_reduce(
                 out=sums_of[image][:, o, SIDE : 2 * SIDE].rearrange("p (l q) -> p l q", q=COMBS)[:, :, 0:combs],
                 in_=over_rows_of[o][:, 0 : combs * COMB].rearrange("p (q i l) -> p l q i", q=combs, i=BAND_ROWS),
@@ -295,12 +313,13 @@ def tile_pam_module_pa_t_kernel(
             if not (0 <= w < BANDS - LAST_BANDS and w % BANDS_PER_IMAGE == BANDS_PER_IMAGE - 1):
                 return
             image = w // BANDS_PER_IMAGE
-            if image not in DERIVED_IMAGES:
+            derived = DERIVED_TILES[image]
+            if derived == 0:
                 return
-            columns = sums_of[image][:, 0:DERIVED, SIDE : 2 * SIDE].rearrange("p o (l q) -> p o l q", q=COMBS)
-            known = out_pool.tile([P, DERIVED, CELLS_PER_ROW], F32)
+            columns = sums_of[image][:, 0:derived, SIDE : 2 * SIDE].rearrange("p o (l q) -> p o l q", q=COMBS)
+            known = out_pool.tile([P, derived, CELLS_PER_ROW], F32)
             nc.vector.tensor_reduce(out=known[:], in_=columns[:, :, :, 0 : COMBS - 1], axis=X_AXIS, op=ADD)
-            together = out_pool.tile([P, DERIVED, CELLS_PER_ROW], F32)
+            together = out_pool.tile([P, derived, CELLS_PER_ROW], F32)
             nc.vector.tensor_reduce(
                 out=together[:], in_=parts_of[image][:].rearrange("p b o l -> p o l b"), axis=X_AXIS, op=ADD
             )
@@ -311,14 +330,15 @@ def tile_pam_module_pa_t_kernel(
                 return
             image = w // BANDS_PER_IMAGE
             pooled = out_pool.tile([P, O_TILES, 2 * SIDE], F32)
-            nc.vector.scalar_tensor_tensor(
-                out=pooled[:],
-                in0=sums_of[image][:],
-                scalar=1.0 / SIDE,
-                in1=bias_cols[:].unsqueeze(2).to_broadcast([P, O_TILES, 2 * SIDE]),
-                op0=MULT,
-                op1=ADD,
-            )
+            for o in range(O_TILES):
+                nc.gpsimd.tensor_scalar(
+                    out=pooled[:, o, :],
+                    in0=sums_of[image][:, o, :],
+                    scalar1=1.0 / SIDE,
+                    scalar2=bias_cols[:, o : o + 1],
+                    op0=MULT,
+                    op1=ADD,
+                )
             nc.sync.dma_start(out=out_q[image], in_=pooled[:, 0, :])
             nc.sync.dma_start(out=out_k[image], in_=pooled[:, 1, :])
             nc.sync.dma_start(out=out_v[image].rearrange("(h p) c -> p h c", p=P), in_=pooled[:, 2:4, :])
@@ -365,7 +385,7 @@ def tile_pam_module_pa_t_kernel(
             if not is_second(w):
                 pool_over_rows(w)
             derive(w - 2)
-            finish(w - 2)
+            finish(w - 3)
 
         for w in range(-REGROUP_AHEAD, BANDS_PER_IMAGE):
             step(w)

@@ -72,6 +72,7 @@ def tile_pam_module_pa_t_kernel(
         over_cols_of = {}
         over_rows_of = {}
         parts_of = {}
+        derivation_of = {}
         sums_of = {}
 
         w_codes = keep.tile([P, O_ALL], U32, align_bytes=256)
@@ -323,12 +324,15 @@ def tile_pam_module_pa_t_kernel(
             nc.vector.tensor_reduce(
                 out=together[:], in_=parts_of[image][:].rearrange("p b o l -> p o l b"), axis=X_AXIS, op=ADD
             )
-            nc.vector.tensor_sub(out=columns[:, :, :, COMBS - 1], in0=together[:], in1=known[:])
+            derivation_of[image] = (columns[:, :, :, COMBS - 1], together, known)
 
         def finish(w):
             if not (0 <= w < BANDS - LAST_BANDS and w % BANDS_PER_IMAGE == BANDS_PER_IMAGE - 1):
                 return
             image = w // BANDS_PER_IMAGE
+            if image in derivation_of:
+                last_comb, together, known = derivation_of[image]
+                nc.gpsimd.tensor_sub(out=last_comb, in0=together[:], in1=known[:])
             pooled = out_pool.tile([P, O_TILES, 2 * SIDE], F32)
             for o in range(O_TILES):
                 nc.gpsimd.tensor_scalar(
@@ -377,15 +381,15 @@ def tile_pam_module_pa_t_kernel(
         def step(w):
             pool_over_cols(w - 1)
             multiply(w)
+            if is_second(w - 1):
+                pool_over_rows(w - 1)
             quantise(w + QUANTISE_AHEAD)
             regroup(w + REGROUP_AHEAD)
             load(w + REGROUP_AHEAD + RAW_BUFS)
-            if is_second(w - 1):
-                pool_over_rows(w - 1)
             if not is_second(w):
                 pool_over_rows(w)
             derive(w - 2)
-            finish(w - 3)
+            finish(w - 5)
 
         for w in range(-REGROUP_AHEAD, BANDS_PER_IMAGE):
             step(w)

@@ -44,8 +44,8 @@ HEAD_VECTOR_PLACES = 42
 HEAD_BANDS = 4
 HALF_PLACES = COMB // 2
 WARM_UP_PASSES = 8
-GPSIMD_PLACES = 32
-GPSIMD_PIECES = 2
+VECTOR_PLACES = 40
+GPSIMD_PLACES = 16
 DERIVED_TILES = (2, 4, 4, 0)
 
 FLOPS = 2 * IMAGES * SIDE * SIDE * CHANNELS * O_ALL
@@ -146,24 +146,29 @@ def tile_pam_module_pa_t_kernel(
             here = slice((w - first_band) * COMB, (w - first_band + 1) * COMB)
             source = raw_of[w][:].rearrange("p t (m q) -> p m t q", q=COMBS)
             target = grouped_of[first_band][:, :, here, :].rearrange("p q m t -> p m t q")
+            meanwhile = max(w - REGROUP_AHEAD, 0) // BANDS_PER_IMAGE
+            by_gpsimd = DERIVED_TILES[meanwhile] == O_TILES
             pieces = HEAD_PIECES if w == 0 else 1
-            places = HEAD_VECTOR_PLACES if w == 0 else HALF_PLACES if w < HEAD_BANDS else GPSIMD_PLACES
+            if w == 0:
+                places = HEAD_VECTOR_PLACES
+            elif w < HEAD_BANDS:
+                places = HALF_PLACES
+            else:
+                places = GPSIMD_PLACES if by_gpsimd else VECTOR_PLACES
             for n in range(pieces):
                 first, end = n * COMB // pieces, (n + 1) * COMB // pieces
                 cut = first + places
-                if w < HEAD_BANDS:
+                if not by_gpsimd:
                     nc.vector.tensor_copy(out=target[:, first:cut], in_=source[:, first:cut])
                 else:
-                    size = GPSIMD_PLACES // GPSIMD_PIECES
-                    for here in (slice(k * size, (k + 1) * size) for k in range(GPSIMD_PIECES)):
-                        nc.gpsimd.tensor_scalar(
-                            out=target[:, here].rearrange("p m t q -> p m q t"),
-                            in0=source[:, here].rearrange("p m t q -> p m q t"),
-                            scalar1=1.0,
-                            scalar2=0.0,
-                            op0=MULT,
-                            op1=ADD,
-                        )
+                    nc.gpsimd.tensor_scalar(
+                        out=target[:, first:cut].rearrange("p m t q -> p m q t"),
+                        in0=source[:, first:cut].rearrange("p m t q -> p m q t"),
+                        scalar1=1.0,
+                        scalar2=0.0,
+                        op0=MULT,
+                        op1=ADD,
+                    )
                 nc.scalar.copy(out=target[:, cut:end], in_=source[:, cut:end])
 
         def quantise(w):

@@ -33,7 +33,7 @@ COMBS = 4
 COMB = BAND // COMBS
 CELLS_PER_ROW = SIDE // COMBS
 
-FIRST_DOUBLE = 4
+FIRST_DOUBLE = 8
 PAIR = 2
 QUANTISE_AHEAD = 3
 REGROUP_AHEAD = 4

@@ -40,12 +40,11 @@ REGROUP_AHEAD = 4
 RAW_BUFS = 6
 LAST_BANDS = 2
 HEAD_PIECES = 2
-HEAD_VECTOR_PLACES = 42
+HEAD_VECTOR_ROWS = 3
 HEAD_BANDS = 4
-HALF_PLACES = COMB // 2
 WARM_UP_PASSES = 8
-VECTOR_PLACES = 40
-GPSIMD_PLACES = 16
+VECTOR_ROWS = 2
+GPSIMD_ROWS = 1
 DERIVED_TILES = (2, 4, 4, 0)
 
 FLOPS = 2 * IMAGES * SIDE * SIDE * CHANNELS * O_ALL
@@ -144,26 +143,26 @@ def tile_pam_module_pa_t_kernel(
             if w == first_band:
                 grouped_of[w] = grouped_pool.tile([P, COMBS, bands * COMB, PACK], BF16, align_bytes=64, name="grouped")
             here = slice((w - first_band) * COMB, (w - first_band + 1) * COMB)
-            source = raw_of[w][:].rearrange("p t (m q) -> p m t q", q=COMBS)
-            target = grouped_of[first_band][:, :, here, :].rearrange("p q m t -> p m t q")
+            source = raw_of[w][:].rearrange("p t (i q l) -> p i q l t", i=BAND_ROWS, q=COMBS)
+            target = grouped_of[first_band][:, :, here, :].rearrange("p q (i l) t -> p i q l t", i=BAND_ROWS)
             meanwhile = max(w - REGROUP_AHEAD, 0) // BANDS_PER_IMAGE
             by_gpsimd = DERIVED_TILES[meanwhile] == O_TILES
             pieces = HEAD_PIECES if w == 0 else 1
             if w == 0:
-                places = HEAD_VECTOR_PLACES
+                rows = HEAD_VECTOR_ROWS
             elif w < HEAD_BANDS:
-                places = HALF_PLACES
+                rows = BAND_ROWS // 2
             else:
-                places = GPSIMD_PLACES if by_gpsimd else VECTOR_PLACES
+                rows = GPSIMD_ROWS if by_gpsimd else VECTOR_ROWS
             for n in range(pieces):
-                first, end = n * COMB // pieces, (n + 1) * COMB // pieces
-                cut = first + places
+                first, end = n * BAND_ROWS // pieces, (n + 1) * BAND_ROWS // pieces
+                cut = first + rows
                 if not by_gpsimd:
                     nc.vector.tensor_copy(out=target[:, first:cut], in_=source[:, first:cut])
                 else:
                     nc.gpsimd.tensor_scalar(
-                        out=target[:, first:cut].rearrange("p m t q -> p m q t"),
-                        in0=source[:, first:cut].rearrange("p m t q -> p m q t"),
+                        out=target[:, first:cut],
+                        in0=source[:, first:cut],
                         scalar1=1.0,
                         scalar2=0.0,
                         op0=MULT,
@@ -300,8 +299,8 @@ def tile_pam_module_pa_t_kernel(
         def pool_tile_over_rows(image, o):
             combs = combs_over_rows(image, o)
             nc.vector.tensor_reduce(
-                out=sums_of[image][:, o, SIDE : 2 * SIDE].rearrange("p (l q) -> p l q", q=COMBS)[:, :, 0:combs],
-                in_=over_rows_of[o][:, 0 : combs * COMB].rearrange("p (q i l) -> p l q i", q=combs, i=BAND_ROWS),
+                out=sums_of[image][:, o, SIDE : 2 * SIDE].rearrange("p (q l) -> p q l", q=COMBS)[:, 0:combs, :],
+                in_=over_rows_of[o][:, 0 : combs * COMB].rearrange("p (q i l) -> p q l i", q=combs, i=BAND_ROWS),
                 axis=X_AXIS,
                 op=ADD,
             )
@@ -322,7 +321,7 @@ def tile_pam_module_pa_t_kernel(
             derived = DERIVED_TILES[image]
             if derived == 0:
                 return
-            columns = sums_of[image][:, 0:derived, SIDE : 2 * SIDE].rearrange("p o (l q) -> p o l q", q=COMBS)
+            columns = sums_of[image][:, 0:derived, SIDE : 2 * SIDE].rearrange("p o (q l) -> p o l q", q=COMBS)
             known = out_pool.tile([P, derived, CELLS_PER_ROW], F32)
             nc.vector.tensor_reduce(out=known[:], in_=columns[:, :, :, 0 : COMBS - 1], axis=X_AXIS, op=ADD)
             together = out_pool.tile([P, derived, CELLS_PER_ROW], F32)

@@ -12,6 +12,7 @@ FP8X4 = mybir.dt.float8_e4m3fn_x4
 ADD = mybir.AluOpType.add
 MULT = mybir.AluOpType.mult
 X_AXIS = mybir.AxisListType.X
+XY_AXES = mybir.AxisListType.XY
 IDENTITY = mybir.ActivationFunctionType.Identity
 
 IMAGES = 4
@@ -33,19 +34,20 @@ COMBS = 4
 COMB = BAND // COMBS
 CELLS_PER_ROW = SIDE // COMBS
 
-FIRST_DOUBLE = 8
+FIRST_DOUBLE = 4
 PAIR = 2
 QUANTISE_AHEAD = 3
 REGROUP_AHEAD = 4
 RAW_BUFS = 6
-LAST_BANDS = 2
+LAST_BANDS = 4
 HEAD_PIECES = 2
-HEAD_VECTOR_ROWS = 3
+HEAD_VECTOR_STRIPS = 3
 HEAD_BANDS = 4
 WARM_UP_PASSES = 8
-VECTOR_ROWS = 2
-GPSIMD_ROWS = 1
-DERIVED_TILES = (2, 4, 4, 0)
+GPSIMD_ROWS = 4
+RUN = 4
+DERIVED_TILES = (4, 4, 4, 3)
+KNOWN = COMBS - 1
 
 FLOPS = 2 * IMAGES * SIDE * SIDE * CHANNELS * O_ALL
 
@@ -71,7 +73,6 @@ def tile_pam_module_pa_t_kernel(
         over_cols_of = {}
         over_rows_of = {}
         parts_of = {}
-        derivation_of = {}
         sums_of = {}
 
         w_codes = keep.tile([P, O_ALL], U32, align_bytes=256)
@@ -113,7 +114,7 @@ def tile_pam_module_pa_t_kernel(
                 nc.tensor.matmul(unused[:], lhsT=zeros[:, 0:P], rhs=zeros[:], start=True, stop=True)
 
         def group_of(w):
-            if FIRST_DOUBLE <= w < BANDS - LAST_BANDS:
+            if w >= FIRST_DOUBLE:
                 return w - (w - FIRST_DOUBLE) % PAIR, PAIR
             return w, 1
 
@@ -136,39 +137,49 @@ def tile_pam_module_pa_t_kernel(
                 )
             raw_of[w] = raw
 
+        def place_of(w, q):
+            first_band, bands = group_of(w)
+            second = w - first_band
+            if q == KNOWN:
+                return KNOWN * bands + second
+            return [k for k in range(second, KNOWN * bands, bands) if k % KNOWN == q][0]
+
+        def copy_strip(engine, w, q, rows):
+            source = raw_of[w][:].rearrange("p t (i q h k) -> p q i h t k", i=BAND_ROWS, q=COMBS, k=RUN)[:, q, rows]
+            target = grouped_of[group_of(w)[0]][:, place_of(w, q)]
+            target = target.rearrange("p (i h k) t -> p i h t k", i=BAND_ROWS, k=RUN)[:, rows]
+            if engine == "vector":
+                nc.vector.tensor_copy(out=target, in_=source)
+            elif engine == "scalar":
+                nc.scalar.copy(out=target, in_=source)
+            else:
+                nc.gpsimd.tensor_scalar(
+                    out=target.rearrange("p i h t k -> p i h k t"),
+                    in0=source.rearrange("p i h t k -> p i h k t"),
+                    scalar1=1.0,
+                    scalar2=0.0,
+                    op0=MULT,
+                    op1=ADD,
+                )
+
         def regroup(w):
             if not 0 <= w < BANDS:
                 return
             first_band, bands = group_of(w)
             if w == first_band:
-                grouped_of[w] = grouped_pool.tile([P, COMBS, bands * COMB, PACK], BF16, align_bytes=64, name="grouped")
-            here = slice((w - first_band) * COMB, (w - first_band + 1) * COMB)
-            source = raw_of[w][:].rearrange("p t (i q l) -> p i q l t", i=BAND_ROWS, q=COMBS)
-            target = grouped_of[first_band][:, :, here, :].rearrange("p q (i l) t -> p i q l t", i=BAND_ROWS)
-            meanwhile = max(w - REGROUP_AHEAD, 0) // BANDS_PER_IMAGE
-            by_gpsimd = DERIVED_TILES[meanwhile] == O_TILES
+                grouped_of[w] = grouped_pool.tile([P, COMBS * bands, COMB, PACK], BF16, align_bytes=64, name="grouped")
             pieces = HEAD_PIECES if w == 0 else 1
-            if w == 0:
-                rows = HEAD_VECTOR_ROWS
-            elif w < HEAD_BANDS:
-                rows = BAND_ROWS // 2
-            else:
-                rows = GPSIMD_ROWS if by_gpsimd else VECTOR_ROWS
             for n in range(pieces):
-                first, end = n * BAND_ROWS // pieces, (n + 1) * BAND_ROWS // pieces
-                cut = first + rows
-                if not by_gpsimd:
-                    nc.vector.tensor_copy(out=target[:, first:cut], in_=source[:, first:cut])
+                rows = slice(n * BAND_ROWS // pieces, (n + 1) * BAND_ROWS // pieces)
+                if w < HEAD_BANDS:
+                    by_vector = HEAD_VECTOR_STRIPS if w == 0 else COMBS // 2
+                    for q in range(COMBS):
+                        copy_strip("vector" if q < by_vector else "scalar", w, q, rows)
                 else:
-                    nc.gpsimd.tensor_scalar(
-                        out=target[:, first:cut],
-                        in0=source[:, first:cut],
-                        scalar1=1.0,
-                        scalar2=0.0,
-                        op0=MULT,
-                        op1=ADD,
-                    )
-                nc.scalar.copy(out=target[:, cut:end], in_=source[:, cut:end])
+                    copy_strip("gpsimd", w, KNOWN, slice(0, GPSIMD_ROWS))
+                    for q in range(KNOWN):
+                        copy_strip("scalar", w, q, rows)
+                    copy_strip("scalar", w, KNOWN, slice(GPSIMD_ROWS, BAND_ROWS))
 
         def quantise(w):
             if not 0 <= w < BANDS:
@@ -178,7 +189,7 @@ def tile_pam_module_pa_t_kernel(
                 return
             codes = mx_pool.tile([P, bands * BAND], U32, align_bytes=256)
             scales = mx_pool.tile([P, bands * BAND], U8, align_bytes=256)
-            values = grouped_of[first_band][:].rearrange("p q m t -> p (q m t)")
+            values = grouped_of[first_band][:].rearrange("p k m t -> p (k m t)")
             pieces = HEAD_PIECES if w == 0 else 1
             width = bands * BAND // pieces
             for n in range(pieces):
@@ -207,32 +218,29 @@ def tile_pam_module_pa_t_kernel(
             bands = range(image * BANDS_PER_IMAGE, (image + 1) * BANDS_PER_IMAGE)
             return [w for w in bands if group_of(w)[0] == w]
 
-        def combs_over_rows(image, o):
-            return COMBS - 1 if o < DERIVED_TILES[image] else COMBS
-
-        def row_passes(bands, combs):
-            if bands == 1 and combs == COMBS:
-                return [(0, 0, BAND)]
+        def row_passes(w, derived):
+            bands = group_of(w)[1]
+            if derived and bands == 1:
+                return [(0, 3, 1), (1, 1, 2)] if w % 2 else [(0, 0, 2), (2, 2, 1)]
+            if derived:
+                return [(0, 0, 4), (4, 1, 2)]
             if bands == 1:
-                return [(0, 0, 2 * COMB), (2 * COMB, 2 * COMB, COMB)]
-            if combs == COMBS:
-                passes = [(COMB, 0, 2 * COMB), (5 * COMB, 2 * COMB, 2 * COMB)]
-                return passes + [(0, 0, COMB), (3 * COMB, COMB, 2 * COMB), (7 * COMB, 3 * COMB, COMB)]
-            return [(COMB, 0, 2 * COMB), (5 * COMB, 2 * COMB, COMB), (0, 0, COMB), (3 * COMB, COMB, 2 * COMB)]
+                return [(0, 0, 4)]
+            return [(0, 0, 2), (5, 2, 2), (2, 2, 1), (3, 0, 2), (7, 3, 1)]
 
         def add_rows(w, o):
-            bands = group_of(w)[1]
+            image = w // BANDS_PER_IMAGE
             image_start = w % BANDS_PER_IMAGE == 0
-            image_end = (w + bands) % BANDS_PER_IMAGE == 0
+            image_end = (w + group_of(w)[1]) % BANDS_PER_IMAGE == 0
             if image_start:
                 over_rows_of[o] = over_rows_psum.tile([P, BAND], F32, name="over_rows")
-            passes = row_passes(bands, combs_over_rows(w // BANDS_PER_IMAGE, o))
-            for n, (first, cell, width) in enumerate(passes):
+            passes = row_passes(w, o < DERIVED_TILES[image])
+            for n, (block, cell, width) in enumerate(passes):
                 one_pass(
-                    over_rows_of[o][:, cell : cell + width],
+                    over_rows_of[o][:, cell * COMB : (cell + width) * COMB],
                     w,
                     o,
-                    slice(first, first + width),
+                    slice(block * COMB, (block + width) * COMB),
                     image_start and n == 0,
                     image_end and n == len(passes) - 1,
                 )
@@ -259,12 +267,18 @@ def tile_pam_module_pa_t_kernel(
                     add_cols(over_cols[:, n, :], first_band, o)
 
         def multiply_last(o):
-            over_cols = over_cols_psum.tile([P, LAST_BANDS, COMB], F32, tag="over_cols")
-            over_cols_of["last", o] = over_cols
-            for w in range(BANDS - LAST_BANDS, BANDS):
-                add_rows(w, o)
-            for n in range(LAST_BANDS):
-                add_cols(over_cols[:, n, :], BANDS - LAST_BANDS + n, o)
+            groups = range(BANDS - LAST_BANDS, BANDS, PAIR)
+            for w in groups:
+                over_cols_of[w, o] = over_cols_psum.tile([P, PAIR * COMB], F32, tag="over_cols", name="over_cols")
+            if o == O_TILES - 1:
+                for w in groups:
+                    add_rows(w, o)
+                for w in groups:
+                    add_cols(over_cols_of[w, o][:], w, o)
+            else:
+                for w in groups:
+                    add_rows(w, o)
+                    add_cols(over_cols_of[w, o][:], w, o)
 
         def pool_over_cols(w):
             if not 0 <= w < BANDS - LAST_BANDS:
@@ -297,12 +311,14 @@ def tile_pam_module_pa_t_kernel(
                 )
 
         def pool_tile_over_rows(image, o):
-            combs = combs_over_rows(image, o)
+            cells = over_rows_of[o][:].rearrange("p (c i l) -> p c l i", c=COMBS, i=BAND_ROWS)
+            columns = sums_of[image][:, o, SIDE : 2 * SIDE].rearrange("p (q l) -> p q l", q=COMBS)
+            if o >= DERIVED_TILES[image]:
+                nc.vector.tensor_reduce(out=columns, in_=cells, axis=X_AXIS, op=ADD)
+                return
+            nc.vector.tensor_reduce(out=columns[:, 1:KNOWN], in_=cells[:, 1:KNOWN], axis=X_AXIS, op=ADD)
             nc.vector.tensor_reduce(
-                out=sums_of[image][:, o, SIDE : 2 * SIDE].rearrange("p (q l) -> p q l", q=COMBS)[:, 0:combs, :],
-                in_=over_rows_of[o][:, 0 : combs * COMB].rearrange("p (q i l) -> p q l i", q=combs, i=BAND_ROWS),
-                axis=X_AXIS,
-                op=ADD,
+                out=columns[:, 0], in_=cells[:, 0 : KNOWN + 1 : KNOWN].rearrange("p c l i -> p l c i"), axis=XY_AXES, op=ADD
             )
 
         def pool_over_rows(w):
@@ -314,29 +330,19 @@ def tile_pam_module_pa_t_kernel(
                 for n in range(tiles):
                     pool_tile_over_rows(w // BANDS_PER_IMAGE, (w - first_band) * tiles + n)
 
-        def derive(w):
-            if not (0 <= w < BANDS - LAST_BANDS and w % BANDS_PER_IMAGE == BANDS_PER_IMAGE - 1):
-                return
-            image = w // BANDS_PER_IMAGE
-            derived = DERIVED_TILES[image]
-            if derived == 0:
-                return
-            columns = sums_of[image][:, 0:derived, SIDE : 2 * SIDE].rearrange("p o (q l) -> p o l q", q=COMBS)
-            known = out_pool.tile([P, derived, CELLS_PER_ROW], F32)
-            nc.vector.tensor_reduce(out=known[:], in_=columns[:, :, :, 0 : COMBS - 1], axis=X_AXIS, op=ADD)
-            together = out_pool.tile([P, derived, CELLS_PER_ROW], F32)
-            nc.vector.tensor_reduce(
-                out=together[:], in_=parts_of[image][:].rearrange("p b o l -> p o l b"), axis=X_AXIS, op=ADD
-            )
-            derivation_of[image] = (columns[:, :, :, COMBS - 1], together, known)
-
         def finish(w):
             if not (0 <= w < BANDS - LAST_BANDS and w % BANDS_PER_IMAGE == BANDS_PER_IMAGE - 1):
                 return
             image = w // BANDS_PER_IMAGE
-            if image in derivation_of:
-                last_comb, together, known = derivation_of[image]
-                nc.gpsimd.tensor_sub(out=last_comb, in0=together[:], in1=known[:])
+            derived = DERIVED_TILES[image]
+            strips = sums_of[image][:, 0:derived, SIDE : 2 * SIDE].rearrange("p o (q l) -> p o q l", q=COMBS)
+            parts = parts_of[image]
+            rest = out_pool.tile([P, derived, CELLS_PER_ROW], F32)
+            nc.gpsimd.tensor_sub(out=rest[:], in0=parts[:, 0], in1=strips[:, :, 0])
+            for n in range(1, len(groups_of(image))):
+                nc.gpsimd.tensor_add(out=rest[:], in0=rest[:], in1=parts[:, n])
+            for q in range(1, KNOWN):
+                nc.gpsimd.tensor_sub(out=strips[:, :, KNOWN] if q == KNOWN - 1 else rest[:], in0=rest[:], in1=strips[:, :, q])
             pooled = out_pool.tile([P, O_TILES, 2 * SIDE], F32)
             for o in range(O_TILES):
                 nc.gpsimd.tensor_scalar(
@@ -353,13 +359,44 @@ def tile_pam_module_pa_t_kernel(
 
         def pool_last(o):
             image = IMAGES - 1
+            derived = o < DERIVED_TILES[image]
+            groups = range(BANDS - LAST_BANDS, BANDS, PAIR)
+
+            def over_cols(w):
+                first_row = (w % BANDS_PER_IMAGE) * BAND_ROWS
+                cells = over_cols_of[w, o][:]
+                nc.vector.tensor_reduce(
+                    out=sums_of[image][:, o, first_row : first_row + PAIR * BAND_ROWS],
+                    in_=cells.rearrange("p (i l) -> p i l", l=CELLS_PER_ROW),
+                    axis=X_AXIS,
+                    op=ADD,
+                )
+                if derived:
+                    nc.vector.tensor_reduce(
+                        out=parts_of[image][:, groups_of(image).index(w), o, :],
+                        in_=cells.rearrange("p (i l) -> p l i", l=CELLS_PER_ROW),
+                        axis=X_AXIS,
+                        op=ADD,
+                    )
+
+            if not derived:
+                pool_tile_over_rows(image, o)
+                for w in groups:
+                    over_cols(w)
+                return
+            over_cols(groups[0])
             pool_tile_over_rows(image, o)
+            over_cols(groups[1])
+            columns = sums_of[image][:, o, SIDE : 2 * SIDE].rearrange("p (q l) -> p q l", q=COMBS)
+            known = out_pool.tile([P, CELLS_PER_ROW], F32)
             nc.vector.tensor_reduce(
-                out=sums_of[image][:, o, SIDE - LAST_BANDS * BAND_ROWS : SIDE],
-                in_=over_cols_of["last", o][:].rearrange("p b (i l) -> p (b i) l", l=CELLS_PER_ROW),
-                axis=X_AXIS,
-                op=ADD,
+                out=known[:], in_=columns[:, 0:KNOWN].rearrange("p q l -> p l q"), axis=X_AXIS, op=ADD
             )
+            together = out_pool.tile([P, CELLS_PER_ROW], F32)
+            nc.vector.tensor_reduce(
+                out=together[:], in_=parts_of[image][:, :, o, :].rearrange("p b l -> p l b"), axis=X_AXIS, op=ADD
+            )
+            nc.vector.tensor_sub(out=columns[:, KNOWN], in0=together[:], in1=known[:])
 
         def finish_last(o):
             image = IMAGES - 1
@@ -392,7 +429,6 @@ def tile_pam_module_pa_t_kernel(
             load(w + REGROUP_AHEAD + RAW_BUFS)
             if not is_second(w):
                 pool_over_rows(w)
-            derive(w - 2)
             finish(w - 5)
 
         for w in range(-REGROUP_AHEAD, BANDS_PER_IMAGE):

@@ -12,7 +12,6 @@ FP8X4 = mybir.dt.float8_e4m3fn_x4
 ADD = mybir.AluOpType.add
 MULT = mybir.AluOpType.mult
 X_AXIS = mybir.AxisListType.X
-XY_AXES = mybir.AxisListType.XY
 IDENTITY = mybir.ActivationFunctionType.Identity
 
 IMAGES = 4
@@ -44,9 +43,8 @@ HEAD_PIECES = 2
 HEAD_VECTOR_STRIPS = 3
 HEAD_BANDS = 4
 WARM_UP_PASSES = 8
-GPSIMD_ROWS = 4
 RUN = 4
-DERIVED_TILES = (4, 4, 4, 3)
+DERIVED_TILES = (2, 4, 4, 3)
 KNOWN = COMBS - 1
 
 FLOPS = 2 * IMAGES * SIDE * SIDE * CHANNELS * O_ALL
@@ -176,10 +174,9 @@ def tile_pam_module_pa_t_kernel(
                     for q in range(COMBS):
                         copy_strip("vector" if q < by_vector else "scalar", w, q, rows)
                 else:
-                    copy_strip("gpsimd", w, KNOWN, slice(0, GPSIMD_ROWS))
+                    copy_strip("gpsimd", w, KNOWN, rows)
                     for q in range(KNOWN):
                         copy_strip("scalar", w, q, rows)
-                    copy_strip("scalar", w, KNOWN, slice(GPSIMD_ROWS, BAND_ROWS))
 
         def quantise(w):
             if not 0 <= w < BANDS:
@@ -311,14 +308,11 @@ def tile_pam_module_pa_t_kernel(
                 )
 
         def pool_tile_over_rows(image, o):
-            cells = over_rows_of[o][:].rearrange("p (c i l) -> p c l i", c=COMBS, i=BAND_ROWS)
-            columns = sums_of[image][:, o, SIDE : 2 * SIDE].rearrange("p (q l) -> p q l", q=COMBS)
-            if o >= DERIVED_TILES[image]:
-                nc.vector.tensor_reduce(out=columns, in_=cells, axis=X_AXIS, op=ADD)
-                return
-            nc.vector.tensor_reduce(out=columns[:, 1:KNOWN], in_=cells[:, 1:KNOWN], axis=X_AXIS, op=ADD)
             nc.vector.tensor_reduce(
-                out=columns[:, 0], in_=cells[:, 0 : KNOWN + 1 : KNOWN].rearrange("p c l i -> p l c i"), axis=XY_AXES, op=ADD
+                out=sums_of[image][:, o, SIDE : 2 * SIDE].rearrange("p (c l) -> p c l", c=COMBS),
+                in_=over_rows_of[o][:].rearrange("p (c i l) -> p c l i", c=COMBS, i=BAND_ROWS),
+                axis=X_AXIS,
+                op=ADD,
             )
 
         def pool_over_rows(w):
@@ -341,8 +335,10 @@ def tile_pam_module_pa_t_kernel(
             nc.gpsimd.tensor_sub(out=rest[:], in0=parts[:, 0], in1=strips[:, :, 0])
             for n in range(1, len(groups_of(image))):
                 nc.gpsimd.tensor_add(out=rest[:], in0=rest[:], in1=parts[:, n])
-            for q in range(1, KNOWN):
-                nc.gpsimd.tensor_sub(out=strips[:, :, KNOWN] if q == KNOWN - 1 else rest[:], in0=rest[:], in1=strips[:, :, q])
+            for c in range(1, COMBS):
+                nc.gpsimd.tensor_sub(out=rest[:], in0=rest[:], in1=strips[:, :, c])
+            nc.gpsimd.tensor_add(out=strips[:, :, 0], in0=strips[:, :, 0], in1=strips[:, :, KNOWN])
+            nc.gpsimd.tensor_scalar(out=strips[:, :, KNOWN], in0=rest[:], scalar1=1.0, scalar2=0.0, op0=MULT, op1=ADD)
             pooled = out_pool.tile([P, O_TILES, 2 * SIDE], F32)
             for o in range(O_TILES):
                 nc.gpsimd.tensor_scalar(
@@ -390,12 +386,13 @@ def tile_pam_module_pa_t_kernel(
             columns = sums_of[image][:, o, SIDE : 2 * SIDE].rearrange("p (q l) -> p q l", q=COMBS)
             known = out_pool.tile([P, CELLS_PER_ROW], F32)
             nc.vector.tensor_reduce(
-                out=known[:], in_=columns[:, 0:KNOWN].rearrange("p q l -> p l q"), axis=X_AXIS, op=ADD
+                out=known[:], in_=columns.rearrange("p q l -> p l q"), axis=X_AXIS, op=ADD
             )
             together = out_pool.tile([P, CELLS_PER_ROW], F32)
             nc.vector.tensor_reduce(
                 out=together[:], in_=parts_of[image][:, :, o, :].rearrange("p b l -> p l b"), axis=X_AXIS, op=ADD
             )
+            nc.vector.tensor_add(out=columns[:, 0], in0=columns[:, 0], in1=columns[:, KNOWN])
             nc.vector.tensor_sub(out=columns[:, KNOWN], in0=together[:], in1=known[:])
 
         def finish_last(o):

@@ -35,17 +35,20 @@ CELLS_PER_ROW = SIDE // COMBS
 
 FIRST_DOUBLE = 4
 PAIR = 2
-QUANTISE_AHEAD = 3
-REGROUP_AHEAD = 4
+QUANTISE_AHEAD = 4
+REGROUP_AHEAD = 5
 RAW_BUFS = 6
 LAST_BANDS = 4
 HEAD_PIECES = 2
 HEAD_VECTOR_STRIPS = 3
 HEAD_BANDS = 4
 WARM_UP_PASSES = 8
+GPSIMD_ROWS = 4
+VECTOR_HELPS_UNTIL = 12
 RUN = 4
 DERIVED_TILES = (2, 4, 4, 3)
 KNOWN = COMBS - 1
+GPSIMD_DERIVES = 2
 
 FLOPS = 2 * IMAGES * SIDE * SIDE * CHANNELS * O_ALL
 
@@ -61,6 +64,7 @@ def tile_pam_module_pa_t_kernel(
         grouped_pool = stack.enter_context(tc.tile_pool(name="grouped", bufs=3))
         mx_pool = stack.enter_context(tc.tile_pool(name="mx", bufs=QUANTISE_AHEAD + 3))
         out_pool = stack.enter_context(tc.tile_pool(name="out", bufs=2))
+        last_pool = stack.enter_context(tc.tile_pool(name="last", bufs=O_TILES))
         over_rows_psum = stack.enter_context(tc.psum_pool(name="over_rows_psum", bufs=5))
         over_cols_psum = stack.enter_context(tc.psum_pool(name="over_cols_psum", bufs=3))
 
@@ -174,9 +178,10 @@ def tile_pam_module_pa_t_kernel(
                     for q in range(COMBS):
                         copy_strip("vector" if q < by_vector else "scalar", w, q, rows)
                 else:
-                    copy_strip("gpsimd", w, KNOWN, rows)
+                    copy_strip("gpsimd", w, KNOWN, slice(0, GPSIMD_ROWS))
                     for q in range(KNOWN):
-                        copy_strip("scalar", w, q, rows)
+                        copy_strip("vector" if q == 0 and w < VECTOR_HELPS_UNTIL else "scalar", w, q, rows)
+                    copy_strip("scalar", w, KNOWN, slice(GPSIMD_ROWS, BAND_ROWS))
 
         def quantise(w):
             if not 0 <= w < BANDS:
@@ -324,21 +329,23 @@ def tile_pam_module_pa_t_kernel(
                 for n in range(tiles):
                     pool_tile_over_rows(w // BANDS_PER_IMAGE, (w - first_band) * tiles + n)
 
-        def finish(w):
-            if not (0 <= w < BANDS - LAST_BANDS and w % BANDS_PER_IMAGE == BANDS_PER_IMAGE - 1):
-                return
-            image = w // BANDS_PER_IMAGE
-            derived = DERIVED_TILES[image]
-            strips = sums_of[image][:, 0:derived, SIDE : 2 * SIDE].rearrange("p o (q l) -> p o q l", q=COMBS)
+        def derive(image, tiles):
+            strips = sums_of[image][:, tiles, SIDE : 2 * SIDE].rearrange("p o (q l) -> p o q l", q=COMBS)
             parts = parts_of[image]
-            rest = out_pool.tile([P, derived, CELLS_PER_ROW], F32)
-            nc.gpsimd.tensor_sub(out=rest[:], in0=parts[:, 0], in1=strips[:, :, 0])
+            rest = out_pool.tile([P, tiles.stop - tiles.start, CELLS_PER_ROW], F32)
+            nc.gpsimd.tensor_sub(out=rest[:], in0=parts[:, 0, tiles], in1=strips[:, :, 0])
             for n in range(1, len(groups_of(image))):
-                nc.gpsimd.tensor_add(out=rest[:], in0=rest[:], in1=parts[:, n])
+                nc.gpsimd.tensor_add(out=rest[:], in0=rest[:], in1=parts[:, n, tiles])
             for c in range(1, COMBS):
                 nc.gpsimd.tensor_sub(out=rest[:], in0=rest[:], in1=strips[:, :, c])
             nc.gpsimd.tensor_add(out=strips[:, :, 0], in0=strips[:, :, 0], in1=strips[:, :, KNOWN])
             nc.gpsimd.tensor_scalar(out=strips[:, :, KNOWN], in0=rest[:], scalar1=1.0, scalar2=0.0, op0=MULT, op1=ADD)
+
+        def finish(w):
+            if not (0 <= w < BANDS - LAST_BANDS and w % BANDS_PER_IMAGE == BANDS_PER_IMAGE - 1):
+                return
+            image = w // BANDS_PER_IMAGE
+            derive(image, slice(0, DERIVED_TILES[image]))
             pooled = out_pool.tile([P, O_TILES, 2 * SIDE], F32)
             for o in range(O_TILES):
                 nc.gpsimd.tensor_scalar(
@@ -383,6 +390,8 @@ def tile_pam_module_pa_t_kernel(
             over_cols(groups[0])
             pool_tile_over_rows(image, o)
             over_cols(groups[1])
+            if o < GPSIMD_DERIVES:
+                return
             columns = sums_of[image][:, o, SIDE : 2 * SIDE].rearrange("p (q l) -> p q l", q=COMBS)
             known = out_pool.tile([P, CELLS_PER_ROW], F32)
             nc.vector.tensor_reduce(
@@ -397,7 +406,7 @@ def tile_pam_module_pa_t_kernel(
 
         def finish_last(o):
             image = IMAGES - 1
-            pooled = out_pool.tile([P, 2 * SIDE], F32, name="pooled_tile")
+            pooled = last_pool.tile([P, 2 * SIDE], F32)
             nc.scalar.activation(
                 out=pooled[:], in_=sums_of[image][:, o, :], func=IDENTITY, bias=bias_cols[:, o : o + 1], scale=1.0 / SIDE
             )
@@ -436,4 +445,9 @@ def tile_pam_module_pa_t_kernel(
         for o in range(O_TILES):
             multiply_last(o)
             pool_last(o)
-            finish_last(o)
+            if o == GPSIMD_DERIVES - 1:
+                derive(IMAGES - 1, slice(0, GPSIMD_DERIVES))
+                for m in range(GPSIMD_DERIVES):
+                    finish_last(m)
+            elif o >= GPSIMD_DERIVES:
+                finish_last(o)

@@ -33,7 +33,7 @@ COMBS = 4
 COMB = BAND // COMBS
 CELLS_PER_ROW = SIDE // COMBS
 
-FIRST_DOUBLE = 4
+FIRST_DOUBLE = 2
 PAIR = 2
 QUANTISE_AHEAD = 4
 REGROUP_AHEAD = 5
@@ -44,9 +44,9 @@ HEAD_VECTOR_STRIPS = 3
 HEAD_BANDS = 4
 WARM_UP_PASSES = 8
 GPSIMD_ROWS = 4
-VECTOR_HELPS_UNTIL = 12
+VECTOR_HELPS_UNTIL = 10
 RUN = 4
-DERIVED_TILES = (2, 4, 4, 3)
+DERIVED_TILES = (4, 4, 4, 3)
 KNOWN = COMBS - 1
 GPSIMD_DERIVES = 2
 
@@ -119,9 +119,6 @@ def tile_pam_module_pa_t_kernel(
             if w >= FIRST_DOUBLE:
                 return w - (w - FIRST_DOUBLE) % PAIR, PAIR
             return w, 1
-
-        def is_second(w):
-            return group_of(w)[0] < w
 
         def load(w):
             if not 0 <= w < BANDS:
@@ -428,13 +425,10 @@ def tile_pam_module_pa_t_kernel(
         def step(w):
             pool_over_cols(w - 1)
             multiply(w)
-            if is_second(w - 1):
-                pool_over_rows(w - 1)
             quantise(w + QUANTISE_AHEAD)
             regroup(w + REGROUP_AHEAD)
             load(w + REGROUP_AHEAD + RAW_BUFS)
-            if not is_second(w):
-                pool_over_rows(w)
+            pool_over_rows(w)
             finish(w - 5)
 
         for w in range(-REGROUP_AHEAD, BANDS_PER_IMAGE):

@@ -43,10 +43,10 @@ HEAD_PIECES = 2
 HEAD_VECTOR_STRIPS = 3
 HEAD_BANDS = 4
 WARM_UP_PASSES = 8
-GPSIMD_ROWS = 4
-VECTOR_HELPS_UNTIL = 10
+HELP_UNTIL = 12
+HALF_ROWS = BAND_ROWS // 2
 RUN = 4
-DERIVED_TILES = (4, 4, 4, 3)
+DERIVED_TILES = (2, 4, 4, 3)
 KNOWN = COMBS - 1
 GPSIMD_DERIVES = 2
 
@@ -175,10 +175,13 @@ def tile_pam_module_pa_t_kernel(
                     for q in range(COMBS):
                         copy_strip("vector" if q < by_vector else "scalar", w, q, rows)
                 else:
-                    copy_strip("gpsimd", w, KNOWN, slice(0, GPSIMD_ROWS))
-                    for q in range(KNOWN):
-                        copy_strip("vector" if q == 0 and w < VECTOR_HELPS_UNTIL else "scalar", w, q, rows)
-                    copy_strip("scalar", w, KNOWN, slice(GPSIMD_ROWS, BAND_ROWS))
+                    helped = w < HELP_UNTIL
+                    for q in range(COMBS):
+                        first = 0
+                        if q == KNOWN and (helped or w == first_band):
+                            first = HALF_ROWS
+                            copy_strip("gpsimd" if helped else "vector", w, q, slice(0, first))
+                        copy_strip("vector" if q == 0 and helped else "scalar", w, q, slice(first, BAND_ROWS))
 
         def quantise(w):
             if not 0 <= w < BANDS:

from contextlib import ExitStack

import concourse.mybir as mybir
from concourse.masks import make_identity

F32 = mybir.dt.float32
BF16 = mybir.dt.bfloat16
I32 = mybir.dt.int32
U32 = mybir.dt.uint32
U8 = mybir.dt.uint8
FP8X4 = mybir.dt.float8_e4m3fn_x4
ADD = mybir.AluOpType.add
MULT = mybir.AluOpType.mult
X_AXIS = mybir.AxisListType.X
IDENTITY = mybir.ActivationFunctionType.Identity

IMAGES = 4
CHANNELS = 512
SIDE = 64
P = 128
PACK = 4
assert CHANNELS == P * PACK

O_TILES = 4
O_ALL = O_TILES * P
SCALE_PITCH = 256

BAND_ROWS = 8
BAND = BAND_ROWS * SIDE
BANDS_PER_IMAGE = SIDE // BAND_ROWS
BANDS = IMAGES * BANDS_PER_IMAGE
COMBS = 4
COMB = BAND // COMBS
CELLS_PER_ROW = SIDE // COMBS

FIRST_DOUBLE = 2
PAIR = 2
QUANTISE_AHEAD = 4
REGROUP_AHEAD = 5
RAW_BUFS = 6
LAST_BANDS = 4
HEAD_PIECES = 2
HEAD_VECTOR_STRIPS = 3
HEAD_BANDS = 4
WARM_UP_PASSES = 8
HELP_UNTIL = 12
HALF_ROWS = BAND_ROWS // 2
RUN = 4
DERIVED_TILES = (2, 4, 4, 3)
KNOWN = COMBS - 1
GPSIMD_DERIVES = 2

FLOPS = 2 * IMAGES * SIDE * SIDE * CHANNELS * O_ALL


def tile_pam_module_pa_t_kernel(
    tc, x, wq_words, wq_scales, bq, wk_words, wk_scales, bk, wv_words, wv_scales, bv, out_q, out_k, out_v
):
    nc = tc.nc
    with ExitStack() as stack:
        stack.enter_context(tc.manual_schedule())
        keep = stack.enter_context(tc.tile_pool(name="keep", bufs=1))
        raw_pool = stack.enter_context(tc.tile_pool(name="raw", bufs=RAW_BUFS))
        grouped_pool = stack.enter_context(tc.tile_pool(name="grouped", bufs=3))
        mx_pool = stack.enter_context(tc.tile_pool(name="mx", bufs=QUANTISE_AHEAD + 3))
        out_pool = stack.enter_context(tc.tile_pool(name="out", bufs=2))
        last_pool = stack.enter_context(tc.tile_pool(name="last", bufs=O_TILES))
        over_rows_psum = stack.enter_context(tc.psum_pool(name="over_rows_psum", bufs=5))
        over_cols_psum = stack.enter_context(tc.psum_pool(name="over_cols_psum", bufs=3))

        raw_of = {}
        grouped_of = {}
        codes_of = {}
        scales_of = {}
        over_cols_of = {}
        over_rows_of = {}
        parts_of = {}
        sums_of = {}

        w_codes = keep.tile([P, O_ALL], U32, align_bytes=256)
        w_scales = keep.tile([P, O_TILES, SCALE_PITCH], U8, align_bytes=256)
        bias_rows = keep.tile([P, P], BF16)
        bias_cols = keep.tile([P, O_TILES], F32)
        identity = keep.tile([P, P], BF16)

        def load_biases():
            nc.vector.memset(bias_rows[:], 0.0)
            nc.sync.dma_start(out=bias_rows[0:1, :], in_=bq.rearrange("(r o) -> r o", r=1))
            nc.sync.dma_start(out=bias_rows[1:2, :], in_=bk.rearrange("(r o) -> r o", r=1))
            nc.sync.dma_start(out=bias_rows[2:4, :], in_=bv.rearrange("(r o) -> r o", r=2))
            make_identity(nc, identity[:])

        def spread_biases():
            transposed = over_cols_psum.tile([P, P], BF16, tag="over_cols")
            nc.tensor.transpose(transposed[:], bias_rows[:], identity[:])
            nc.vector.tensor_copy(out=bias_cols[:], in_=transposed[:, 0:O_TILES])

        def load_weight(words, scales, first):
            cols = slice(first, first + words.shape[2])
            tiles = slice(first // P, (first + words.shape[2]) // P)
            nc.sync.dma_start(
                out=w_codes[:, cols].bitcast(I32),
                in_=words[0].rearrange("p n t -> p (n t)").bitcast(I32),
            )
            for quadrant in range(4):
                nc.sync.dma_start(
                    out=w_scales[32 * quadrant : 32 * quadrant + 4, tiles, 0:P].bitcast(I32),
                    in_=scales[0, 4 * quadrant : 4 * quadrant + 4, :].bitcast(I32).rearrange("r (o n) -> r o n", n=P // 4),
                )

        def warm_up():
            zeros = keep.tile([P, BAND], BF16)
            nc.vector.memset(zeros[:], 0.0)
            unused = over_cols_psum.tile([P, BAND], F32, tag="over_cols")
            for n in range(WARM_UP_PASSES):
                nc.tensor.matmul(unused[:], lhsT=zeros[:, 0:P], rhs=zeros[:], start=True, stop=True)

        def group_of(w):
            if w >= FIRST_DOUBLE:
                return w - (w - FIRST_DOUBLE) % PAIR, PAIR
            return w, 1

        def load(w):
            if not 0 <= w < BANDS:
                return
            image, band = divmod(w, BANDS_PER_IMAGE)
            raw = raw_pool.tile([P, PACK, BAND], BF16)
            pieces = HEAD_PIECES if w == 0 else 1
            rows = BAND_ROWS // pieces
            for n in range(pieces):
                first = band * BAND_ROWS + n * rows
                queue = nc.scalar if w == 0 else nc.gpsimd if w < HEAD_BANDS else nc.sync
                queue.dma_start(
                    out=raw[:, :, n * rows * SIDE : (n + 1) * rows * SIDE],
                    in_=x[image, :, first : first + rows, :].rearrange("(p t) i j -> p t (i j)", t=PACK),
                )
            raw_of[w] = raw

        def place_of(w, q):
            first_band, bands = group_of(w)
            second = w - first_band
            if q == KNOWN:
                return KNOWN * bands + second
            return [k for k in range(second, KNOWN * bands, bands) if k % KNOWN == q][0]

        def copy_strip(engine, w, q, rows):
            source = raw_of[w][:].rearrange("p t (i q h k) -> p q i h t k", i=BAND_ROWS, q=COMBS, k=RUN)[:, q, rows]
            target = grouped_of[group_of(w)[0]][:, place_of(w, q)]
            target = target.rearrange("p (i h k) t -> p i h t k", i=BAND_ROWS, k=RUN)[:, rows]
            if engine == "vector":
                nc.vector.tensor_copy(out=target, in_=source)
            elif engine == "scalar":
                nc.scalar.copy(out=target, in_=source)
            else:
                nc.gpsimd.tensor_scalar(
                    out=target.rearrange("p i h t k -> p i h k t"),
                    in0=source.rearrange("p i h t k -> p i h k t"),
                    scalar1=1.0,
                    scalar2=0.0,
                    op0=MULT,
                    op1=ADD,
                )

        def regroup(w):
            if not 0 <= w < BANDS:
                return
            first_band, bands = group_of(w)
            if w == first_band:
                grouped_of[w] = grouped_pool.tile([P, COMBS * bands, COMB, PACK], BF16, align_bytes=64, name="grouped")
            pieces = HEAD_PIECES if w == 0 else 1
            for n in range(pieces):
                rows = slice(n * BAND_ROWS // pieces, (n + 1) * BAND_ROWS // pieces)
                if w < HEAD_BANDS:
                    by_vector = HEAD_VECTOR_STRIPS if w == 0 else COMBS // 2
                    for q in range(COMBS):
                        copy_strip("vector" if q < by_vector else "scalar", w, q, rows)
                else:
                    helped = w < HELP_UNTIL
                    for q in range(COMBS):
                        first = 0
                        if q == KNOWN and (helped or w == first_band):
                            first = HALF_ROWS
                            copy_strip("gpsimd" if helped else "vector", w, q, slice(0, first))
                        copy_strip("vector" if q == 0 and helped else "scalar", w, q, slice(first, BAND_ROWS))

        def quantise(w):
            if not 0 <= w < BANDS:
                return
            first_band, bands = group_of(w)
            if w != first_band + bands - 1:
                return
            codes = mx_pool.tile([P, bands * BAND], U32, align_bytes=256)
            scales = mx_pool.tile([P, bands * BAND], U8, align_bytes=256)
            values = grouped_of[first_band][:].rearrange("p k m t -> p (k m t)")
            pieces = HEAD_PIECES if w == 0 else 1
            width = bands * BAND // pieces
            for n in range(pieces):
                here = slice(n * width, (n + 1) * width)
                nc.vector.quantize_mx(
                    out=codes[:, here].bitcast(FP8X4),
                    scales=scales[:, here],
                    in_=values[:, n * width * PACK : (n + 1) * width * PACK],
                )
            codes_of[first_band] = codes
            scales_of[first_band] = scales

        def one_pass(out, w, o, pixels, start, stop):
            outputs = slice(o * P, (o + 1) * P)
            nc.tensor.matmul_mx(
                out=out,
                lhsT=w_codes[:, outputs].bitcast(FP8X4),
                lhsT_scale=w_scales[:, o, 0:P],
                rhs=codes_of[w][:, pixels].bitcast(FP8X4),
                rhs_scale=scales_of[w][:, pixels],
                start=start,
                stop=stop,
            )

        def groups_of(image):
            bands = range(image * BANDS_PER_IMAGE, (image + 1) * BANDS_PER_IMAGE)
            return [w for w in bands if group_of(w)[0] == w]

        def row_passes(w, derived):
            bands = group_of(w)[1]
            if derived and bands == 1:
                return [(0, 3, 1), (1, 1, 2)] if w % 2 else [(0, 0, 2), (2, 2, 1)]
            if derived:
                return [(0, 0, 4), (4, 1, 2)]
            if bands == 1:
                return [(0, 0, 4)]
            return [(0, 0, 2), (5, 2, 2), (2, 2, 1), (3, 0, 2), (7, 3, 1)]

        def add_rows(w, o):
            image = w // BANDS_PER_IMAGE
            image_start = w % BANDS_PER_IMAGE == 0
            image_end = (w + group_of(w)[1]) % BANDS_PER_IMAGE == 0
            if image_start:
                over_rows_of[o] = over_rows_psum.tile([P, BAND], F32, name="over_rows")
            passes = row_passes(w, o < DERIVED_TILES[image])
            for n, (block, cell, width) in enumerate(passes):
                one_pass(
                    over_rows_of[o][:, cell * COMB : (cell + width) * COMB],
                    w,
                    o,
                    slice(block * COMB, (block + width) * COMB),
                    image_start and n == 0,
                    image_end and n == len(passes) - 1,
                )

        def add_cols(out, w, o):
            comb = group_of(w)[1] * COMB
            for q in range(COMBS):
                one_pass(out, w, o, slice(q * comb, (q + 1) * comb), q == 0, q == COMBS - 1)

        def multiply(w):
            if not 0 <= w < BANDS - LAST_BANDS:
                return
            first_band, bands = group_of(w)
            tiles = O_TILES // bands
            over_cols = over_cols_psum.tile([P, tiles, bands * COMB], F32, tag="over_cols")
            over_cols_of[w] = over_cols
            for n in range(tiles):
                o = (w - first_band) * tiles + n
                if w == 0:
                    add_cols(over_cols[:, n, :], first_band, o)
                    add_rows(first_band, o)
                else:
                    add_rows(first_band, o)
                    add_cols(over_cols[:, n, :], first_band, o)

        def multiply_last(o):
            groups = range(BANDS - LAST_BANDS, BANDS, PAIR)
            for w in groups:
                over_cols_of[w, o] = over_cols_psum.tile([P, PAIR * COMB], F32, tag="over_cols", name="over_cols")
            if o == O_TILES - 1:
                for w in groups:
                    add_rows(w, o)
                for w in groups:
                    add_cols(over_cols_of[w, o][:], w, o)
            else:
                for w in groups:
                    add_rows(w, o)
                    add_cols(over_cols_of[w, o][:], w, o)

        def pool_over_cols(w):
            if not 0 <= w < BANDS - LAST_BANDS:
                return
            image, band = divmod(w, BANDS_PER_IMAGE)
            first_band, bands = group_of(w)
            if band == 0:
                sums_of[image] = out_pool.tile([P, O_TILES, 2 * SIDE], F32, name="sums")
            tiles = O_TILES // bands
            first_tile = (w - first_band) * tiles
            first_row = (first_band % BANDS_PER_IMAGE) * BAND_ROWS
            nc.vector.tensor_reduce(
                out=sums_of[image][:, first_tile : first_tile + tiles, first_row : first_row + bands * BAND_ROWS],
                in_=over_cols_of[w][:].rearrange("p o (i l) -> p o i l", l=CELLS_PER_ROW),
                axis=X_AXIS,
                op=ADD,
            )
            derived = min(DERIVED_TILES[image] - first_tile, tiles)
            if derived > 0:
                groups = groups_of(image)
                if band == 0:
                    parts_of[image] = out_pool.tile(
                        [P, len(groups), DERIVED_TILES[image], CELLS_PER_ROW], F32, name="parts"
                    )
                nc.vector.tensor_reduce(
                    out=parts_of[image][:, groups.index(first_band), first_tile : first_tile + derived, :],
                    in_=over_cols_of[w][:, 0:derived, :].rearrange("p o (i l) -> p o l i", l=CELLS_PER_ROW),
                    axis=X_AXIS,
                    op=ADD,
                )

        def pool_tile_over_rows(image, o):
            nc.vector.tensor_reduce(
                out=sums_of[image][:, o, SIDE : 2 * SIDE].rearrange("p (c l) -> p c l", c=COMBS),
                in_=over_rows_of[o][:].rearrange("p (c i l) -> p c l i", c=COMBS, i=BAND_ROWS),
                axis=X_AXIS,
                op=ADD,
            )

        def pool_over_rows(w):
            if not 0 <= w < BANDS - LAST_BANDS:
                return
            first_band, bands = group_of(w)
            if (first_band + bands) % BANDS_PER_IMAGE == 0:
                tiles = O_TILES // bands
                for n in range(tiles):
                    pool_tile_over_rows(w // BANDS_PER_IMAGE, (w - first_band) * tiles + n)

        def derive(image, tiles):
            strips = sums_of[image][:, tiles, SIDE : 2 * SIDE].rearrange("p o (q l) -> p o q l", q=COMBS)
            parts = parts_of[image]
            rest = out_pool.tile([P, tiles.stop - tiles.start, CELLS_PER_ROW], F32)
            nc.gpsimd.tensor_sub(out=rest[:], in0=parts[:, 0, tiles], in1=strips[:, :, 0])
            for n in range(1, len(groups_of(image))):
                nc.gpsimd.tensor_add(out=rest[:], in0=rest[:], in1=parts[:, n, tiles])
            for c in range(1, COMBS):
                nc.gpsimd.tensor_sub(out=rest[:], in0=rest[:], in1=strips[:, :, c])
            nc.gpsimd.tensor_add(out=strips[:, :, 0], in0=strips[:, :, 0], in1=strips[:, :, KNOWN])
            nc.gpsimd.tensor_scalar(out=strips[:, :, KNOWN], in0=rest[:], scalar1=1.0, scalar2=0.0, op0=MULT, op1=ADD)

        def finish(w):
            if not (0 <= w < BANDS - LAST_BANDS and w % BANDS_PER_IMAGE == BANDS_PER_IMAGE - 1):
                return
            image = w // BANDS_PER_IMAGE
            derive(image, slice(0, DERIVED_TILES[image]))
            pooled = out_pool.tile([P, O_TILES, 2 * SIDE], F32)
            for o in range(O_TILES):
                nc.gpsimd.tensor_scalar(
                    out=pooled[:, o, :],
                    in0=sums_of[image][:, o, :],
                    scalar1=1.0 / SIDE,
                    scalar2=bias_cols[:, o : o + 1],
                    op0=MULT,
                    op1=ADD,
                )
            nc.sync.dma_start(out=out_q[image], in_=pooled[:, 0, :])
            nc.sync.dma_start(out=out_k[image], in_=pooled[:, 1, :])
            nc.sync.dma_start(out=out_v[image].rearrange("(h p) c -> p h c", p=P), in_=pooled[:, 2:4, :])

        def pool_last(o):
            image = IMAGES - 1
            derived = o < DERIVED_TILES[image]
            groups = range(BANDS - LAST_BANDS, BANDS, PAIR)

            def over_cols(w):
                first_row = (w % BANDS_PER_IMAGE) * BAND_ROWS
                cells = over_cols_of[w, o][:]
                nc.vector.tensor_reduce(
                    out=sums_of[image][:, o, first_row : first_row + PAIR * BAND_ROWS],
                    in_=cells.rearrange("p (i l) -> p i l", l=CELLS_PER_ROW),
                    axis=X_AXIS,
                    op=ADD,
                )
                if derived:
                    nc.vector.tensor_reduce(
                        out=parts_of[image][:, groups_of(image).index(w), o, :],
                        in_=cells.rearrange("p (i l) -> p l i", l=CELLS_PER_ROW),
                        axis=X_AXIS,
                        op=ADD,
                    )

            if not derived:
                pool_tile_over_rows(image, o)
                for w in groups:
                    over_cols(w)
                return
            over_cols(groups[0])
            pool_tile_over_rows(image, o)
            over_cols(groups[1])
            if o < GPSIMD_DERIVES:
                return
            columns = sums_of[image][:, o, SIDE : 2 * SIDE].rearrange("p (q l) -> p q l", q=COMBS)
            known = out_pool.tile([P, CELLS_PER_ROW], F32)
            nc.vector.tensor_reduce(
                out=known[:], in_=columns.rearrange("p q l -> p l q"), axis=X_AXIS, op=ADD
            )
            together = out_pool.tile([P, CELLS_PER_ROW], F32)
            nc.vector.tensor_reduce(
                out=together[:], in_=parts_of[image][:, :, o, :].rearrange("p b l -> p l b"), axis=X_AXIS, op=ADD
            )
            nc.vector.tensor_add(out=columns[:, 0], in0=columns[:, 0], in1=columns[:, KNOWN])
            nc.vector.tensor_sub(out=columns[:, KNOWN], in0=together[:], in1=known[:])

        def finish_last(o):
            image = IMAGES - 1
            pooled = last_pool.tile([P, 2 * SIDE], F32)
            nc.scalar.activation(
                out=pooled[:], in_=sums_of[image][:, o, :], func=IDENTITY, bias=bias_cols[:, o : o + 1], scale=1.0 / SIDE
            )
            target = (out_q[image], out_k[image], out_v[image, 0:P, :], out_v[image, P : 2 * P, :])[o]
            nc.sync.dma_start(out=target, in_=pooled[:])

        warm_up()
        nc.vector.memset(w_scales[:].rearrange("p o n -> p (o n)").bitcast(I32), 0)
        load(0)
        load_weight(wq_words, wq_scales, 0)
        for w in range(1, HEAD_BANDS):
            load(w)
        load_weight(wk_words, wk_scales, P)
        load_weight(wv_words, wv_scales, 2 * P)
        for w in range(HEAD_BANDS, RAW_BUFS):
            load(w)
        load_biases()

        def step(w):
            pool_over_cols(w - 1)
            multiply(w)
            quantise(w + QUANTISE_AHEAD)
            regroup(w + REGROUP_AHEAD)
            load(w + REGROUP_AHEAD + RAW_BUFS)
            pool_over_rows(w)
            finish(w - 5)

        for w in range(-REGROUP_AHEAD, BANDS_PER_IMAGE):
            step(w)
        spread_biases()
        for w in range(BANDS_PER_IMAGE, BANDS - LAST_BANDS + 1):
            step(w)
        for o in range(O_TILES):
            multiply_last(o)
            pool_last(o)
            if o == GPSIMD_DERIVES - 1:
                derive(IMAGES - 1, slice(0, GPSIMD_DERIVES))
                for m in range(GPSIMD_DERIVES):
                    finish_last(m)
            elif o >= GPSIMD_DERIVES:
                finish_last(o)
